import numpy as np
import ml_dtypes

BF16 = ml_dtypes.bfloat16


def bf(x):
    return np.asarray(x, np.float32).astype(BF16)


def f32(x):
    return np.asarray(x, np.float32)


def f64(x):
    return np.asarray(x).astype(np.float64)


def striped(idx):
    return np.tile(idx.reshape(-1, 16).T, (8, 1))


C, S, N = 1024, 1024, 512
EPS = 1e-8
W_SCALE = 0.02


def rmsnorm_cols(v):
    return v / (np.sqrt((v ** 2).mean(axis=0, keepdims=True)) + EPS)


def setup_inputs():
    emb = np.random.standard_normal((C, S)) * np.random.uniform(0.5, 1.5, (1, S))
    hidden = np.random.standard_normal((C, N)) * np.random.uniform(0.5, 1.5, (1, N))
    w_fut = W_SCALE * np.random.standard_normal((C, C))
    w_hid = W_SCALE * np.random.standard_normal((C, C))
    b = 0.1 * np.random.standard_normal((C, 1))
    idx = np.random.permutation(np.tile(np.arange(S), 2))[:N]
    return {"emb": f32(emb), "hidden": f32(hidden), "w_fut": bf(w_fut), "w_hid": bf(w_hid), "b": f32(b), "offs": striped(idx)}


def reference(emb, hidden, w_fut, w_hid, b, offs):
    idx = offs[:16].T.reshape(-1)
    p = f64(w_fut).T @ rmsnorm_cols(f64(emb))
    q = f64(w_hid).T @ rmsnorm_cols(f64(hidden)) + f64(b)
    return p[:, idx] + q

@@ -1,0 +1,121 @@
+import concourse.mybir as mybir
+
+F32 = mybir.dt.float32
+BF16 = mybir.dt.bfloat16
+U16 = mybir.dt.uint16
+ACT = mybir.ActivationFunctionType
+ALU = mybir.AluOpType
+
+PARTS = 128
+CHANNELS = 1024
+WORDS = 1024
+POSITIONS = 512
+BLOCKS = CHANNELS // PARTS
+GROUP = 512
+EPS = 1e-8
+
+FLOPS = 2 * CHANNELS * CHANNELS * (WORDS + POSITIONS)
+
+
+def load_columns(nc, pool, source, first_column, label):
+    raw = []
+    for k in range(BLOCKS):
+        block = pool.tile([PARTS, GROUP], F32, name=f"raw_{label}_{k}")
+        nc.sync.dma_start(
+            block[:], source[k * PARTS : (k + 1) * PARTS, first_column : first_column + GROUP]
+        )
+        raw.append(block)
+    return raw
+
+
+def load_weights(nc, pool, source, label):
+    weights = []
+    for k in range(BLOCKS):
+        block = pool.tile([PARTS, CHANNELS], BF16, name=f"w_{label}_{k}")
+        nc.sync.dma_start(block[:], source[k * PARTS : (k + 1) * PARTS, :])
+        weights.append(block)
+    return weights
+
+
+def normalise(nc, held, work, sums, ones, raw, label):
+    total = work.tile([PARTS, GROUP], F32, name="total")
+    nc.scalar.activation(total[:], raw[0][:], ACT.Square)
+    for k in range(1, BLOCKS):
+        squares = work.tile([PARTS, GROUP], F32, name="squares")
+        nc.scalar.activation(squares[:], raw[k][:], ACT.Square)
+        nc.vector.tensor_tensor(total[:], total[:], squares[:], ALU.add)
+    column_sums = sums.tile([PARTS, GROUP], F32, name="column_sums")
+    nc.tensor.matmul(column_sums[:], ones[:], total[:], start=True, stop=True)
+    rms = work.tile([PARTS, GROUP], F32, name="rms")
+    nc.scalar.activation(rms[:], column_sums[:], ACT.Sqrt, scale=1.0 / CHANNELS)
+    nc.vector.tensor_scalar_add(rms[:], rms[:], EPS)
+    inverse = work.tile([PARTS, GROUP], F32, name="inverse")
+    nc.vector.reciprocal(inverse[:], rms[:])
+    normal = []
+    for k in range(BLOCKS):
+        block = held.tile([PARTS, GROUP], BF16, name=f"normal_{label}_{k}")
+        nc.vector.tensor_tensor(block[:], raw[k][:], inverse[:], ALU.mult)
+        normal.append(block)
+    return normal
+
+
+def project(nc, banks, weights, normal, m):
+    bank = banks.tile([PARTS, GROUP], F32, name="bank")
+    for k in range(BLOCKS):
+        nc.tensor.matmul(
+            bank[:],
+            weights[k][:, m * PARTS : (m + 1) * PARTS],
+            normal[k][:],
+            start=(k == 0),
+            stop=(k == BLOCKS - 1),
+        )
+    return bank
+
+
+def tile_mtp_kernel(tc, emb, hidden, w_fut, w_hid, b, offs, out):
+    nc = tc.nc
+    with (
+        tc.tile_pool(name="held", bufs=1) as held,
+        tc.tile_pool(name="work", bufs=3) as work,
+        tc.psum_pool(name="sums", bufs=2) as sums,
+        tc.psum_pool(name="banks", bufs=6) as banks,
+    ):
+        raw_hidden = load_columns(nc, held, hidden, 0, "hidden")
+        offsets = held.tile([PARTS, POSITIONS // 16], U16, name="offsets")
+        nc.sync.dma_start(offsets[:], offs)
+        weights_hid = load_weights(nc, held, w_hid, "hid")
+        raw_emb = [load_columns(nc, held, emb, 0, "emb0")]
+        bias = held.tile([PARTS, BLOCKS], F32, name="bias")
+        with nc.allow_non_contiguous_dma(reason="1,024 single floats, one for each output channel"):
+            nc.gpsimd.dma_start(bias[:], b.rearrange("(m p) o -> p (m o)", p=PARTS))
+        weights_fut = load_weights(nc, held, w_fut, "fut")
+        raw_emb.append(load_columns(nc, held, emb, GROUP, "emb1"))
+
+        ones = held.tile([PARTS, PARTS], F32, name="ones")
+        nc.vector.memset(ones[:], 1.0)
+
+        normal_hidden = normalise(nc, held, work, sums, ones, raw_hidden, "hidden")
+        normal_emb = [normalise(nc, held, work, sums, ones, raw_emb[0], "emb0")]
+
+        q_blocks = []
+        for m in range(BLOCKS):
+            bank = project(nc, banks, weights_hid, normal_hidden, m)
+            q_block = held.tile([PARTS, POSITIONS], F32, name=f"q_{m}")
+            nc.scalar.activation(q_block[:], bank[:], ACT.Identity, bias=bias[:, m : m + 1])
+            q_blocks.append(q_block)
+
+        normal_emb.append(normalise(nc, held, work, sums, ones, raw_emb[1], "emb1"))
+
+        p_blocks = [held.tile([PARTS, WORDS], F32, name=f"p_{m}") for m in range(BLOCKS)]
+        for half in range(WORDS // GROUP):
+            for m in range(BLOCKS):
+                bank = project(nc, banks, weights_fut, normal_emb[half], m)
+                nc.scalar.activation(
+                    p_blocks[m][:, half * GROUP : (half + 1) * GROUP], bank[:], ACT.Copy
+                )
+                if half == WORDS // GROUP - 1:
+                    merged = work.tile([PARTS, POSITIONS], F32, name="merged")
+                    nc.vector.tensor_tensor(
+                        merged[:], p_blocks[m][:].indirect(offsets[:]), q_blocks[m][:], ALU.add
+                    )
+                    nc.sync.dma_start(out[m * PARTS : (m + 1) * PARTS, :], merged[:])

@@ -1,4 +1,5 @@
 import concourse.mybir as mybir
+from concourse.masks import make_identity
 
 F32 = mybir.dt.float32
 BF16 = mybir.dt.bfloat16
@@ -12,6 +13,7 @@ WORDS = 1024
 POSITIONS = 512
 BLOCKS = CHANNELS // PARTS
 GROUP = 512
+TURNS = GROUP // PARTS
 EPS = 1e-8
 
 FLOPS = 2 * CHANNELS * CHANNELS * (WORDS + POSITIONS)
@@ -37,20 +39,34 @@ def load_weights(nc, pool, source, label):
     return weights
 
 
-def normalise(nc, held, work, sums, ones, raw, label):
+def normalise(nc, held, work, sums, ones, identity, raw, label):
     total = work.tile([PARTS, GROUP], F32, name="total")
     nc.scalar.activation(total[:], raw[0][:], ACT.Square)
     for k in range(1, BLOCKS):
         squares = work.tile([PARTS, GROUP], F32, name="squares")
         nc.scalar.activation(squares[:], raw[k][:], ACT.Square)
         nc.vector.tensor_tensor(total[:], total[:], squares[:], ALU.add)
-    column_sums = sums.tile([PARTS, GROUP], F32, name="column_sums")
-    nc.tensor.matmul(column_sums[:], ones[:], total[:], start=True, stop=True)
-    rms = work.tile([PARTS, GROUP], F32, name="rms")
+    column_sums = sums.tile([PARTS, TURNS], F32, name="column_sums")
+    for t in range(TURNS):
+        nc.tensor.matmul(
+            column_sums[:, t : t + 1],
+            total[:, t * PARTS : (t + 1) * PARTS],
+            ones[:, 0:1],
+            start=True,
+            stop=True,
+        )
+    rms = work.tile([PARTS, TURNS], F32, name="rms")
     nc.scalar.activation(rms[:], column_sums[:], ACT.Sqrt, scale=1.0 / CHANNELS)
     nc.vector.tensor_scalar_add(rms[:], rms[:], EPS)
-    inverse = work.tile([PARTS, GROUP], F32, name="inverse")
-    nc.vector.reciprocal(inverse[:], rms[:])
+    turned_inverse = work.tile([PARTS, TURNS], F32, name="turned_inverse")
+    nc.vector.reciprocal(turned_inverse[:], rms[:])
+    diagonal = work.tile([PARTS, GROUP], F32, name="diagonal")
+    for t in range(TURNS):
+        nc.vector.tensor_scalar_mul(
+            diagonal[:, t * PARTS : (t + 1) * PARTS], identity[:], turned_inverse[:, t : t + 1]
+        )
+    inverse = sums.tile([PARTS, GROUP], F32, name="inverse")
+    nc.tensor.matmul(inverse[:], ones[:], diagonal[:], start=True, stop=True)
     normal = []
     for k in range(BLOCKS):
         block = held.tile([PARTS, GROUP], BF16, name=f"normal_{label}_{k}")
@@ -77,7 +93,7 @@ def tile_mtp_kernel(tc, emb, hidden, w_fut, w_hid, b, offs, out):
     with (
         tc.tile_pool(name="held", bufs=1) as held,
         tc.tile_pool(name="work", bufs=3) as work,
-        tc.psum_pool(name="sums", bufs=2) as sums,
+        tc.psum_pool(name="sums", bufs=1) as sums,
         tc.psum_pool(name="banks", bufs=6) as banks,
     ):
         raw_hidden = load_columns(nc, held, hidden, 0, "hidden")
@@ -93,9 +109,11 @@ def tile_mtp_kernel(tc, emb, hidden, w_fut, w_hid, b, offs, out):
 
         ones = held.tile([PARTS, PARTS], F32, name="ones")
         nc.vector.memset(ones[:], 1.0)
+        identity = held.tile([PARTS, PARTS], F32, name="identity")
+        make_identity(nc, identity[:])
 
-        normal_hidden = normalise(nc, held, work, sums, ones, raw_hidden, "hidden")
-        normal_emb = [normalise(nc, held, work, sums, ones, raw_emb[0], "emb0")]
+        normal_hidden = normalise(nc, held, work, sums, ones, identity, raw_hidden, "hidden")
+        normal_emb = [normalise(nc, held, work, sums, ones, identity, raw_emb[0], "emb0")]
 
         q_blocks = []
         for m in range(BLOCKS):
@@ -104,7 +122,7 @@ def tile_mtp_kernel(tc, emb, hidden, w_fut, w_hid, b, offs, out):
             nc.scalar.activation(q_block[:], bank[:], ACT.Identity, bias=bias[:, m : m + 1])
             q_blocks.append(q_block)
 
-        normal_emb.append(normalise(nc, held, work, sums, ones, raw_emb[1], "emb1"))
+        normal_emb.append(normalise(nc, held, work, sums, ones, identity, raw_emb[1], "emb1"))
 
         p_blocks = [held.tile([PARTS, WORDS], F32, name=f"p_{m}") for m in range(BLOCKS)]
         for half in range(WORDS // GROUP):

@@ -1,5 +1,4 @@
 import concourse.mybir as mybir
-from concourse.masks import make_identity
 
 F32 = mybir.dt.float32
 BF16 = mybir.dt.bfloat16
@@ -12,20 +11,18 @@ CHANNELS = 1024
 WORDS = 1024
 POSITIONS = 512
 BLOCKS = CHANNELS // PARTS
-GROUP = 512
-TURNS = GROUP // PARTS
+BANKS = 6
+SET = BANKS // 2
 EPS = 1e-8
 
 FLOPS = 2 * CHANNELS * CHANNELS * (WORDS + POSITIONS)
 
 
-def load_columns(nc, pool, source, first_column, label):
+def load_columns(nc, pool, source, first, width, label):
     raw = []
     for k in range(BLOCKS):
-        block = pool.tile([PARTS, GROUP], F32, name=f"raw_{label}_{k}")
-        nc.sync.dma_start(
-            block[:], source[k * PARTS : (k + 1) * PARTS, first_column : first_column + GROUP]
-        )
+        block = pool.tile([PARTS, width], F32, name=f"raw_{label}_{k}")
+        nc.sync.dma_start(block[:], source[k * PARTS : (k + 1) * PARTS, first : first + width])
         raw.append(block)
     return raw
 
@@ -39,53 +36,49 @@ def load_weights(nc, pool, source, label):
     return weights
 
 
-def normalise(nc, held, work, sums, ones, identity, raw, label):
-    total = work.tile([PARTS, GROUP], F32, name="total")
+def sum_squares(nc, work, raw, width):
+    total = work.tile([PARTS, width], F32, name="total")
     nc.scalar.activation(total[:], raw[0][:], ACT.Square)
     for k in range(1, BLOCKS):
-        squares = work.tile([PARTS, GROUP], F32, name="squares")
+        squares = work.tile([PARTS, width], F32, name="squares")
         nc.scalar.activation(squares[:], raw[k][:], ACT.Square)
         nc.vector.tensor_tensor(total[:], total[:], squares[:], ALU.add)
-    column_sums = sums.tile([PARTS, TURNS], F32, name="column_sums")
-    for t in range(TURNS):
-        nc.tensor.matmul(
-            column_sums[:, t : t + 1],
-            total[:, t * PARTS : (t + 1) * PARTS],
-            ones[:, 0:1],
-            start=True,
-            stop=True,
-        )
-    rms = work.tile([PARTS, TURNS], F32, name="rms")
+    return total
+
+
+def inverse_norms(nc, work, sums, ones, total, width):
+    column_sums = sums.tile([PARTS, width], F32, name="column_sums")
+    nc.tensor.matmul(column_sums[:], ones[:], total[:], start=True, stop=True)
+    rms = work.tile([PARTS, width], F32, name="rms")
     nc.scalar.activation(rms[:], column_sums[:], ACT.Sqrt, scale=1.0 / CHANNELS)
     nc.vector.tensor_scalar_add(rms[:], rms[:], EPS)
-    turned_inverse = work.tile([PARTS, TURNS], F32, name="turned_inverse")
-    nc.vector.reciprocal(turned_inverse[:], rms[:])
-    diagonal = work.tile([PARTS, GROUP], F32, name="diagonal")
-    for t in range(TURNS):
-        nc.vector.tensor_scalar_mul(
-            diagonal[:, t * PARTS : (t + 1) * PARTS], identity[:], turned_inverse[:, t : t + 1]
-        )
-    inverse = sums.tile([PARTS, GROUP], F32, name="inverse")
-    nc.tensor.matmul(inverse[:], ones[:], diagonal[:], start=True, stop=True)
+    inverse = work.tile([PARTS, width], F32, name="inverse")
+    nc.vector.reciprocal(inverse[:], rms[:])
+    return inverse
+
+
+def scale_columns(nc, held, raw, inverse, width, label):
     normal = []
     for k in range(BLOCKS):
-        block = held.tile([PARTS, GROUP], BF16, name=f"normal_{label}_{k}")
+        block = held.tile([PARTS, width], BF16, name=f"normal_{label}_{k}")
         nc.vector.tensor_tensor(block[:], raw[k][:], inverse[:], ALU.mult)
         normal.append(block)
     return normal
 
 
-def project(nc, banks, weights, normal, m):
-    bank = banks.tile([PARTS, GROUP], F32, name="bank")
+def project(nc, banks, weights, normal, width, first, together):
+    members = range(first, min(first + together, BLOCKS))
+    products = {m: banks.tile([PARTS, width], F32, name="bank") for m in members}
     for k in range(BLOCKS):
-        nc.tensor.matmul(
-            bank[:],
-            weights[k][:, m * PARTS : (m + 1) * PARTS],
-            normal[k][:],
-            start=(k == 0),
-            stop=(k == BLOCKS - 1),
-        )
-    return bank
+        for m in members:
+            nc.tensor.matmul(
+                products[m][:],
+                weights[k][:, m * PARTS : (m + 1) * PARTS],
+                normal[k][:],
+                start=(k == 0),
+                stop=(k == BLOCKS - 1),
+            )
+    return products
 
 
 def tile_mtp_kernel(tc, emb, hidden, w_fut, w_hid, b, offs, out):
@@ -93,47 +86,64 @@ def tile_mtp_kernel(tc, emb, hidden, w_fut, w_hid, b, offs, out):
     with (
         tc.tile_pool(name="held", bufs=1) as held,
         tc.tile_pool(name="work", bufs=3) as work,
-        tc.psum_pool(name="sums", bufs=1) as sums,
-        tc.psum_pool(name="banks", bufs=6) as banks,
+        tc.psum_pool(name="sums", bufs=2) as sums,
+        tc.psum_pool(name="banks", bufs=BANKS) as banks,
     ):
-        raw_hidden = load_columns(nc, held, hidden, 0, "hidden")
+        q_blocks = [held.tile([PARTS, POSITIONS], F32, name=f"q_{m}") for m in range(BLOCKS)]
+        p_blocks = [held.tile([PARTS, WORDS], F32, name=f"p_{m}") for m in range(BLOCKS)]
+
+        half_q, half_p = POSITIONS // 2, WORDS // 2
+        raw_a = load_columns(nc, held, hidden, 0, half_q, "hidden0")
+        raw_b = load_columns(nc, held, hidden, half_q, half_q, "hidden1")
+        weights_hid = load_weights(nc, held, w_hid, "hid")
         offsets = held.tile([PARTS, POSITIONS // 16], U16, name="offsets")
         nc.sync.dma_start(offsets[:], offs)
-        weights_hid = load_weights(nc, held, w_hid, "hid")
-        raw_emb = [load_columns(nc, held, emb, 0, "emb0")]
+        raw_c = load_columns(nc, held, emb, 0, half_p, "emb0")
+        weights_fut = load_weights(nc, held, w_fut, "fut")
+        raw_d = load_columns(nc, held, emb, half_p, half_p, "emb1")
         bias = held.tile([PARTS, BLOCKS], F32, name="bias")
         with nc.allow_non_contiguous_dma(reason="1,024 single floats, one for each output channel"):
             nc.gpsimd.dma_start(bias[:], b.rearrange("(m p) o -> p (m o)", p=PARTS))
-        weights_fut = load_weights(nc, held, w_fut, "fut")
-        raw_emb.append(load_columns(nc, held, emb, GROUP, "emb1"))
+
+        groups = [
+            ("hidden0", raw_a, 0, half_q, weights_hid, q_blocks),
+            ("hidden1", raw_b, half_q, half_q, weights_hid, q_blocks),
+            ("emb0", raw_c, 0, half_p, weights_fut, p_blocks),
+            ("emb1", raw_d, half_p, half_p, weights_fut, p_blocks),
+        ]
 
         ones = held.tile([PARTS, PARTS], F32, name="ones")
         nc.vector.memset(ones[:], 1.0)
-        identity = held.tile([PARTS, PARTS], F32, name="identity")
-        make_identity(nc, identity[:])
 
-        normal_hidden = normalise(nc, held, work, sums, ones, identity, raw_hidden, "hidden")
-        normal_emb = [normalise(nc, held, work, sums, ones, identity, raw_emb[0], "emb0")]
+        label, raw, first, width, weights, target = groups[0]
+        total = sum_squares(nc, work, raw, width)
+        inverse = inverse_norms(nc, work, sums, ones, total, width)
+        normal = scale_columns(nc, held, raw, inverse, width, label)
 
-        q_blocks = []
-        for m in range(BLOCKS):
-            bank = project(nc, banks, weights_hid, normal_hidden, m)
-            q_block = held.tile([PARTS, POSITIONS], F32, name=f"q_{m}")
-            nc.scalar.activation(q_block[:], bank[:], ACT.Identity, bias=bias[:, m : m + 1])
-            q_blocks.append(q_block)
-
-        normal_emb.append(normalise(nc, held, work, sums, ones, identity, raw_emb[1], "emb1"))
-
-        p_blocks = [held.tile([PARTS, WORDS], F32, name=f"p_{m}") for m in range(BLOCKS)]
-        for half in range(WORDS // GROUP):
-            for m in range(BLOCKS):
-                bank = project(nc, banks, weights_fut, normal_emb[half], m)
-                nc.scalar.activation(
-                    p_blocks[m][:, half * GROUP : (half + 1) * GROUP], bank[:], ACT.Copy
-                )
-                if half == WORDS // GROUP - 1:
-                    merged = work.tile([PARTS, POSITIONS], F32, name="merged")
-                    nc.vector.tensor_tensor(
-                        merged[:], p_blocks[m][:].indirect(offsets[:]), q_blocks[m][:], ALU.add
-                    )
-                    nc.sync.dma_start(out[m * PARTS : (m + 1) * PARTS, :], merged[:])
+        for g, (label, raw, first, width, weights, target) in enumerate(groups):
+            last_group = g == len(groups) - 1
+            together = 1 if last_group else SET
+            for step, first_block in enumerate(range(0, BLOCKS, together)):
+                if not last_group:
+                    next_label, next_raw, next_first, next_width, next_weights, next_target = groups[g + 1]
+                    if step == 0:
+                        total = sum_squares(nc, work, next_raw, next_width)
+                    if step == 1:
+                        inverse = inverse_norms(nc, work, sums, ones, total, next_width)
+                    if step == 2:
+                        next_normal = scale_columns(nc, held, next_raw, inverse, next_width, next_label)
+                products = project(nc, banks, weights, normal, width, first_block, together)
+                for m, bank in products.items():
+                    columns = target[m][:, first : first + width]
+                    if target is q_blocks:
+                        nc.scalar.activation(columns, bank[:], ACT.Identity, bias=bias[:, m : m + 1])
+                    else:
+                        nc.scalar.activation(columns, bank[:], ACT.Copy)
+                    if last_group:
+                        merged = work.tile([PARTS, POSITIONS], F32, name="merged")
+                        nc.vector.tensor_tensor(
+                            merged[:], p_blocks[m][:].indirect(offsets[:]), q_blocks[m][:], ALU.add
+                        )
+                        nc.sync.dma_start(out[m * PARTS : (m + 1) * PARTS, :], merged[:])
+            if not last_group:
+                normal = next_normal

@@ -13,6 +13,7 @@ POSITIONS = 512
 BLOCKS = CHANNELS // PARTS
 BANKS = 6
 SET = BANKS // 2
+GROUP = 512
 EPS = 1e-8
 
 FLOPS = 2 * CHANNELS * CHANNELS * (WORDS + POSITIONS)
@@ -92,47 +93,56 @@ def tile_mtp_kernel(tc, emb, hidden, w_fut, w_hid, b, offs, out):
         q_blocks = [held.tile([PARTS, POSITIONS], F32, name=f"q_{m}") for m in range(BLOCKS)]
         p_blocks = [held.tile([PARTS, WORDS], F32, name=f"p_{m}") for m in range(BLOCKS)]
 
-        half_q, half_p = POSITIONS // 2, WORDS // 2
-        raw_a = load_columns(nc, held, hidden, 0, half_q, "hidden0")
-        raw_b = load_columns(nc, held, hidden, half_q, half_q, "hidden1")
+        raw_hidden = load_columns(nc, held, hidden, 0, GROUP, "hidden")
         weights_hid = load_weights(nc, held, w_hid, "hid")
         offsets = held.tile([PARTS, POSITIONS // 16], U16, name="offsets")
         nc.sync.dma_start(offsets[:], offs)
-        raw_c = load_columns(nc, held, emb, 0, half_p, "emb0")
+        raw_emb0 = load_columns(nc, held, emb, 0, GROUP, "emb0")
         weights_fut = load_weights(nc, held, w_fut, "fut")
-        raw_d = load_columns(nc, held, emb, half_p, half_p, "emb1")
+        raw_emb1 = load_columns(nc, held, emb, GROUP, GROUP, "emb1")
         bias = held.tile([PARTS, BLOCKS], F32, name="bias")
         with nc.allow_non_contiguous_dma(reason="1,024 single floats, one for each output channel"):
             nc.gpsimd.dma_start(bias[:], b.rearrange("(m p) o -> p (m o)", p=PARTS))
 
         groups = [
-            ("hidden0", raw_a, 0, half_q, weights_hid, q_blocks),
-            ("hidden1", raw_b, half_q, half_q, weights_hid, q_blocks),
-            ("emb0", raw_c, 0, half_p, weights_fut, p_blocks),
-            ("emb1", raw_d, half_p, half_p, weights_fut, p_blocks),
+            ("hidden", raw_hidden, 0, GROUP, weights_hid, q_blocks),
+            ("emb0", raw_emb0, 0, GROUP, weights_fut, p_blocks),
+            ("emb1", raw_emb1, GROUP, GROUP, weights_fut, p_blocks),
         ]
 
         ones = held.tile([PARTS, PARTS], F32, name="ones")
         nc.vector.memset(ones[:], 1.0)
 
-        label, raw, first, width, weights, target = groups[0]
-        total = sum_squares(nc, work, raw, width)
-        inverse = inverse_norms(nc, work, sums, ones, total, width)
-        normal = scale_columns(nc, held, raw, inverse, width, label)
+        totals, inverses, normals = {}, {}, {}
+        steps = [(g, step) for g in range(len(groups)) for step in range(3)]
+
+        def take_step():
+            g, step = steps.pop(0)
+            label, raw, first, width, weights, target = groups[g]
+            if step == 0:
+                totals[g] = sum_squares(nc, work, raw, width)
+            if step == 1:
+                inverses[g] = inverse_norms(nc, work, sums, ones, totals[g], width)
+            if step == 2:
+                normals[g] = scale_columns(nc, held, raw, inverses[g], width, label)
+
+        take_step()
+        take_step()
+        filler = held.tile([PARTS, GROUP], BF16, name="filler")
+        nc.vector.tensor_copy(filler[:], totals[0][:])
+        unread = banks.tile([PARTS, GROUP], F32, name="bank")
+        for i in range(16):
+            nc.tensor.matmul(unread[:], filler[:, 0:PARTS], filler[:], start=True, stop=True)
+        take_step()
+        take_step()
 
         for g, (label, raw, first, width, weights, target) in enumerate(groups):
             last_group = g == len(groups) - 1
             together = 1 if last_group else SET
-            for step, first_block in enumerate(range(0, BLOCKS, together)):
-                if not last_group:
-                    next_label, next_raw, next_first, next_width, next_weights, next_target = groups[g + 1]
-                    if step == 0:
-                        total = sum_squares(nc, work, next_raw, next_width)
-                    if step == 1:
-                        inverse = inverse_norms(nc, work, sums, ones, total, next_width)
-                    if step == 2:
-                        next_normal = scale_columns(nc, held, next_raw, inverse, next_width, next_label)
-                products = project(nc, banks, weights, normal, width, first_block, together)
+            for first_block in range(0, BLOCKS, together):
+                if steps:
+                    take_step()
+                products = project(nc, banks, weights, normals[g], width, first_block, together)
                 for m, bank in products.items():
                     columns = target[m][:, first : first + width]
                     if target is q_blocks:
@@ -145,5 +155,3 @@ def tile_mtp_kernel(tc, emb, hidden, w_fut, w_hid, b, offs, out):
                             merged[:], p_blocks[m][:].indirect(offsets[:]), q_blocks[m][:], ALU.add
                         )
                         nc.sync.dma_start(out[m * PARTS : (m + 1) * PARTS, :], merged[:])
-            if not last_group:
-                normal = next_normal

@@ -1,4 +1,5 @@
 import concourse.mybir as mybir
+from concourse.masks import make_identity
 
 F32 = mybir.dt.float32
 BF16 = mybir.dt.bfloat16
@@ -11,75 +12,58 @@ CHANNELS = 1024
 WORDS = 1024
 POSITIONS = 512
 BLOCKS = CHANNELS // PARTS
-BANKS = 6
-SET = BANKS // 2
 GROUP = 512
 EPS = 1e-8
 
 FLOPS = 2 * CHANNELS * CHANNELS * (WORDS + POSITIONS)
 
 
-def load_columns(nc, pool, source, first, width, label):
-    raw = []
-    for k in range(BLOCKS):
-        block = pool.tile([PARTS, width], F32, name=f"raw_{label}_{k}")
-        nc.sync.dma_start(block[:], source[k * PARTS : (k + 1) * PARTS, first : first + width])
-        raw.append(block)
-    return raw
+def load_blocks(nc, pool, source, first_column, width, blocks_a_load, label):
+    by_block = source.rearrange("(k p) c -> p k c", p=PARTS)
+    views = []
+    for i, k in enumerate(range(0, BLOCKS, blocks_a_load)):
+        loaded = pool.tile([PARTS, blocks_a_load, width], source.dtype, name=f"{label}_{k}")
+        queue = (nc.sync, nc.scalar)[i % 2]
+        queue.dma_start(
+            loaded[:], by_block[:, k : k + blocks_a_load, first_column : first_column + width]
+        )
+        views += [loaded[:, j, :] for j in range(blocks_a_load)]
+    return views
 
 
-def load_weights(nc, pool, source, label):
-    weights = []
-    for k in range(BLOCKS):
-        block = pool.tile([PARTS, CHANNELS], BF16, name=f"w_{label}_{k}")
-        nc.sync.dma_start(block[:], source[k * PARTS : (k + 1) * PARTS, :])
-        weights.append(block)
-    return weights
-
-
-def sum_squares(nc, work, raw, width):
-    total = work.tile([PARTS, width], F32, name="total")
-    nc.scalar.activation(total[:], raw[0][:], ACT.Square)
+def normalise(nc, held, work, sums, ones, raw, label):
+    total = work.tile([PARTS, GROUP], F32, name="total")
+    nc.scalar.activation(total[:], raw[0], ACT.Square)
     for k in range(1, BLOCKS):
-        squares = work.tile([PARTS, width], F32, name="squares")
-        nc.scalar.activation(squares[:], raw[k][:], ACT.Square)
+        squares = work.tile([PARTS, GROUP], F32, name="squares")
+        nc.scalar.activation(squares[:], raw[k], ACT.Square)
         nc.vector.tensor_tensor(total[:], total[:], squares[:], ALU.add)
-    return total
-
-
-def inverse_norms(nc, work, sums, ones, total, width):
-    column_sums = sums.tile([PARTS, width], F32, name="column_sums")
+    column_sums = sums.tile([PARTS, GROUP], F32, name="column_sums")
     nc.tensor.matmul(column_sums[:], ones[:], total[:], start=True, stop=True)
-    rms = work.tile([PARTS, width], F32, name="rms")
+    rms = work.tile([PARTS, GROUP], F32, name="rms")
     nc.scalar.activation(rms[:], column_sums[:], ACT.Sqrt, scale=1.0 / CHANNELS)
     nc.vector.tensor_scalar_add(rms[:], rms[:], EPS)
-    inverse = work.tile([PARTS, width], F32, name="inverse")
+    inverse = work.tile([PARTS, GROUP], F32, name="inverse")
     nc.vector.reciprocal(inverse[:], rms[:])
-    return inverse
-
-
-def scale_columns(nc, held, raw, inverse, width, label):
     normal = []
     for k in range(BLOCKS):
-        block = held.tile([PARTS, width], BF16, name=f"normal_{label}_{k}")
-        nc.vector.tensor_tensor(block[:], raw[k][:], inverse[:], ALU.mult)
+        block = held.tile([PARTS, GROUP], BF16, name=f"normal_{label}_{k}")
+        nc.vector.tensor_tensor(block[:], raw[k], inverse[:], ALU.mult)
         normal.append(block)
     return normal
 
 
-def project(nc, banks, weights, normal, width, first, together):
-    members = range(first, min(first + together, BLOCKS))
-    products = {m: banks.tile([PARTS, width], F32, name="bank") for m in members}
+def project(nc, banks, weights, normal, m):
+    bank = banks.tile([PARTS, GROUP], F32, name="bank")
     for k in range(BLOCKS):
-        for m in members:
-            nc.tensor.matmul(
-                products[m][:],
-                weights[k][:, m * PARTS : (m + 1) * PARTS],
-                normal[k][:],
-                start=(k == 0),
-                stop=(k == BLOCKS - 1),
-            )
-    return products
+        nc.tensor.matmul(
+            bank[:],
+            weights[k][:, m * PARTS : (m + 1) * PARTS],
+            normal[k][:],
+            start=(k == 0),
+            stop=(k == BLOCKS - 1),
+        )
+    return bank
 
 
 def tile_mtp_kernel(tc, emb, hidden, w_fut, w_hid, b, offs, out):
@@ -88,70 +72,50 @@ def tile_mtp_kernel(tc, emb, hidden, w_fut, w_hid, b, offs, out):
         tc.tile_pool(name="held", bufs=1) as held,
         tc.tile_pool(name="work", bufs=3) as work,
         tc.psum_pool(name="sums", bufs=2) as sums,
-        tc.psum_pool(name="banks", bufs=BANKS) as banks,
+        tc.psum_pool(name="banks", bufs=6) as banks,
     ):
-        q_blocks = [held.tile([PARTS, POSITIONS], F32, name=f"q_{m}") for m in range(BLOCKS)]
-        p_blocks = [held.tile([PARTS, WORDS], F32, name=f"p_{m}") for m in range(BLOCKS)]
-
-        raw_hidden = load_columns(nc, held, hidden, 0, GROUP, "hidden")
-        weights_hid = load_weights(nc, held, w_hid, "hid")
+        raw_hidden = load_blocks(nc, held, hidden, 0, GROUP, 1, "hidden")
+        b_rows = held.tile([BLOCKS, PARTS], F32, name="b_rows")
+        nc.sync.dma_start(b_rows[:], b.rearrange("(m p) o -> m (p o)", p=PARTS))
+        weights_hid = load_blocks(nc, held, w_hid, 0, CHANNELS, BLOCKS // 2, "w_hid")
+        raw_emb = [load_blocks(nc, held, emb, 0, GROUP, BLOCKS // 2, "emb0")]
+        weights_fut = load_blocks(nc, held, w_fut, 0, CHANNELS, BLOCKS // 2, "w_fut")
+        raw_emb.append(load_blocks(nc, held, emb, GROUP, GROUP, BLOCKS // 2, "emb1"))
         offsets = held.tile([PARTS, POSITIONS // 16], U16, name="offsets")
         nc.sync.dma_start(offsets[:], offs)
-        raw_emb0 = load_columns(nc, held, emb, 0, GROUP, "emb0")
-        weights_fut = load_weights(nc, held, w_fut, "fut")
-        raw_emb1 = load_columns(nc, held, emb, GROUP, GROUP, "emb1")
-        bias = held.tile([PARTS, BLOCKS], F32, name="bias")
-        with nc.allow_non_contiguous_dma(reason="1,024 single floats, one for each output channel"):
-            nc.gpsimd.dma_start(bias[:], b.rearrange("(m p) o -> p (m o)", p=PARTS))
-
-        groups = [
-            ("hidden", raw_hidden, 0, GROUP, weights_hid, q_blocks),
-            ("emb0", raw_emb0, 0, GROUP, weights_fut, p_blocks),
-            ("emb1", raw_emb1, GROUP, GROUP, weights_fut, p_blocks),
-        ]
 
         ones = held.tile([PARTS, PARTS], F32, name="ones")
         nc.vector.memset(ones[:], 1.0)
 
-        totals, inverses, normals = {}, {}, {}
-        steps = [(g, step) for g in range(len(groups)) for step in range(3)]
+        identity = held.tile([BLOCKS, BLOCKS], F32, name="identity")
+        make_identity(nc, identity[:])
+        turned = banks.tile([PARTS, BLOCKS], F32, name="bank")
+        nc.tensor.matmul(turned[:], b_rows[:], identity[:], start=True, stop=True)
+        bias = held.tile([PARTS, BLOCKS], F32, name="bias")
+        nc.vector.tensor_copy(bias[:], turned[:])
 
-        def take_step():
-            g, step = steps.pop(0)
-            label, raw, first, width, weights, target = groups[g]
-            if step == 0:
-                totals[g] = sum_squares(nc, work, raw, width)
-            if step == 1:
-                inverses[g] = inverse_norms(nc, work, sums, ones, totals[g], width)
-            if step == 2:
-                normals[g] = scale_columns(nc, held, raw, inverses[g], width, label)
+        normal_hidden = normalise(nc, held, work, sums, ones, raw_hidden, "hidden")
+        normal_emb = [normalise(nc, held, work, sums, ones, raw_emb[0], "emb0")]
 
-        take_step()
-        take_step()
-        filler = held.tile([PARTS, GROUP], BF16, name="filler")
-        nc.vector.tensor_copy(filler[:], totals[0][:])
-        unread = banks.tile([PARTS, GROUP], F32, name="bank")
-        for i in range(16):
-            nc.tensor.matmul(unread[:], filler[:, 0:PARTS], filler[:], start=True, stop=True)
-        take_step()
-        take_step()
+        q_blocks = []
+        for m in range(BLOCKS):
+            bank = project(nc, banks, weights_hid, normal_hidden, m)
+            q_block = held.tile([PARTS, POSITIONS], F32, name=f"q_{m}")
+            nc.scalar.activation(q_block[:], bank[:], ACT.Identity, bias=bias[:, m : m + 1])
+            q_blocks.append(q_block)
 
-        for g, (label, raw, first, width, weights, target) in enumerate(groups):
-            last_group = g == len(groups) - 1
-            together = 1 if last_group else SET
-            for first_block in range(0, BLOCKS, together):
-                if steps:
-                    take_step()
-                products = project(nc, banks, weights, normals[g], width, first_block, together)
-                for m, bank in products.items():
-                    columns = target[m][:, first : first + width]
-                    if target is q_blocks:
-                        nc.scalar.activation(columns, bank[:], ACT.Identity, bias=bias[:, m : m + 1])
-                    else:
-                        nc.scalar.activation(columns, bank[:], ACT.Copy)
-                    if last_group:
-                        merged = work.tile([PARTS, POSITIONS], F32, name="merged")
-                        nc.vector.tensor_tensor(
-                            merged[:], p_blocks[m][:].indirect(offsets[:]), q_blocks[m][:], ALU.add
-                        )
-                        nc.sync.dma_start(out[m * PARTS : (m + 1) * PARTS, :], merged[:])
+        normal_emb.append(normalise(nc, held, work, sums, ones, raw_emb[1], "emb1"))
+
+        p_blocks = [held.tile([PARTS, WORDS], F32, name=f"p_{m}") for m in range(BLOCKS)]
+        for half in range(WORDS // GROUP):
+            for m in range(BLOCKS):
+                bank = project(nc, banks, weights_fut, normal_emb[half], m)
+                nc.scalar.activation(
+                    p_blocks[m][:, half * GROUP : (half + 1) * GROUP], bank[:], ACT.Copy
+                )
+                if half == WORDS // GROUP - 1:
+                    merged = work.tile([PARTS, POSITIONS], F32, name="merged")
+                    nc.vector.tensor_tensor(
+                        merged[:], p_blocks[m][:].indirect(offsets[:]), q_blocks[m][:], ALU.add
+                    )
+                    nc.sync.dma_start(out[m * PARTS : (m + 1) * PARTS, :], merged[:])

@@ -18,25 +18,32 @@ EPS = 1e-8
 FLOPS = 2 * CHANNELS * CHANNELS * (WORDS + POSITIONS)
 
 
-def load_blocks(nc, pool, source, first_column, width, blocks_a_load, label):
-    by_block = source.rearrange("(k p) c -> p k c", p=PARTS)
-    views = []
-    for i, k in enumerate(range(0, BLOCKS, blocks_a_load)):
-        loaded = pool.tile([PARTS, blocks_a_load, width], source.dtype, name=f"{label}_{k}")
-        queue = (nc.sync, nc.scalar)[i % 2]
-        queue.dma_start(
-            loaded[:], by_block[:, k : k + blocks_a_load, first_column : first_column + width]
+def load_columns(nc, pool, source, first_column, label):
+    raw = []
+    for k in range(BLOCKS):
+        block = pool.tile([PARTS, GROUP], F32, name=f"raw_{label}_{k}")
+        nc.sync.dma_start(
+            block[:], source[k * PARTS : (k + 1) * PARTS, first_column : first_column + GROUP]
         )
-        views += [loaded[:, j, :] for j in range(blocks_a_load)]
-    return views
+        raw.append(block)
+    return raw
+
+
+def load_weights(nc, pool, source, label):
+    weights = []
+    for k in range(BLOCKS):
+        block = pool.tile([PARTS, CHANNELS], BF16, name=f"w_{label}_{k}")
+        nc.sync.dma_start(block[:], source[k * PARTS : (k + 1) * PARTS, :])
+        weights.append(block)
+    return weights
 
 
 def normalise(nc, held, work, sums, ones, raw, label):
     total = work.tile([PARTS, GROUP], F32, name="total")
-    nc.scalar.activation(total[:], raw[0], ACT.Square)
+    nc.scalar.activation(total[:], raw[0][:], ACT.Square)
     for k in range(1, BLOCKS):
         squares = work.tile([PARTS, GROUP], F32, name="squares")
-        nc.scalar.activation(squares[:], raw[k], ACT.Square)
+        nc.scalar.activation(squares[:], raw[k][:], ACT.Square)
         nc.vector.tensor_tensor(total[:], total[:], squares[:], ALU.add)
     column_sums = sums.tile([PARTS, GROUP], F32, name="column_sums")
     nc.tensor.matmul(column_sums[:], ones[:], total[:], start=True, stop=True)
@@ -48,7 +55,7 @@ def normalise(nc, held, work, sums, ones, raw, label):
     normal = []
     for k in range(BLOCKS):
         block = held.tile([PARTS, GROUP], BF16, name=f"normal_{label}_{k}")
-        nc.vector.tensor_tensor(block[:], raw[k], inverse[:], ALU.mult)
+        nc.vector.tensor_tensor(block[:], raw[k][:], inverse[:], ALU.mult)
         normal.append(block)
     return normal
 
@@ -74,15 +81,15 @@ def tile_mtp_kernel(tc, emb, hidden, w_fut, w_hid, b, offs, out):
         tc.psum_pool(name="sums", bufs=2) as sums,
         tc.psum_pool(name="banks", bufs=6) as banks,
     ):
-        raw_hidden = load_blocks(nc, held, hidden, 0, GROUP, 1, "hidden")
-        b_rows = held.tile([BLOCKS, PARTS], F32, name="b_rows")
-        nc.sync.dma_start(b_rows[:], b.rearrange("(m p) o -> m (p o)", p=PARTS))
-        weights_hid = load_blocks(nc, held, w_hid, 0, CHANNELS, BLOCKS // 2, "w_hid")
-        raw_emb = [load_blocks(nc, held, emb, 0, GROUP, BLOCKS // 2, "emb0")]
-        weights_fut = load_blocks(nc, held, w_fut, 0, CHANNELS, BLOCKS // 2, "w_fut")
-        raw_emb.append(load_blocks(nc, held, emb, GROUP, GROUP, BLOCKS // 2, "emb1"))
+        raw_hidden = load_columns(nc, held, hidden, 0, "hidden")
         offsets = held.tile([PARTS, POSITIONS // 16], U16, name="offsets")
         nc.sync.dma_start(offsets[:], offs)
+        b_rows = held.tile([BLOCKS, PARTS], F32, name="b_rows")
+        nc.sync.dma_start(b_rows[:], b.rearrange("(m p) o -> m (p o)", p=PARTS))
+        weights_hid = load_weights(nc, held, w_hid, "hid")
+        raw_emb = [load_columns(nc, held, emb, 0, "emb0")]
+        weights_fut = load_weights(nc, held, w_fut, "fut")
+        raw_emb.append(load_columns(nc, held, emb, GROUP, "emb1"))
 
         ones = held.tile([PARTS, PARTS], F32, name="ones")
         nc.vector.memset(ones[:], 1.0)

@@ -12,19 +12,23 @@ CHANNELS = 1024
 WORDS = 1024
 POSITIONS = 512
 BLOCKS = CHANNELS // PARTS
-GROUP = 512
 EPS = 1e-8
+
+THIRD = WORDS // 3 // 16 * 16
+FIRST_THIRD = WORDS - 2 * THIRD
+
+WORK_BUFS = 3
+SUM_BANKS = 2
+PRODUCT_BANKS = 8 - SUM_BANKS
 
 FLOPS = 2 * CHANNELS * CHANNELS * (WORDS + POSITIONS)
 
 
-def load_columns(nc, pool, source, first_column, label):
+def load_columns(nc, pool, source, first, width, label):
     raw = []
     for k in range(BLOCKS):
-        block = pool.tile([PARTS, GROUP], F32, name=f"raw_{label}_{k}")
-        nc.sync.dma_start(
-            block[:], source[k * PARTS : (k + 1) * PARTS, first_column : first_column + GROUP]
-        )
+        block = pool.tile([PARTS, width], F32, name=f"raw_{label}_{k}")
+        nc.sync.dma_start(block[:], source[k * PARTS : (k + 1) * PARTS, first : first + width])
         raw.append(block)
     return raw
 
@@ -38,30 +42,30 @@ def load_weights(nc, pool, source, label):
     return weights
 
 
-def normalise(nc, held, work, sums, ones, raw, label):
-    total = work.tile([PARTS, GROUP], F32, name="total")
+def normalise(nc, held, work, sums, ones, raw, width, label):
+    total = work.tile([PARTS, width], F32, name="total")
     nc.scalar.activation(total[:], raw[0][:], ACT.Square)
     for k in range(1, BLOCKS):
-        squares = work.tile([PARTS, GROUP], F32, name="squares")
+        squares = work.tile([PARTS, width], F32, name="squares")
         nc.scalar.activation(squares[:], raw[k][:], ACT.Square)
         nc.vector.tensor_tensor(total[:], total[:], squares[:], ALU.add)
-    column_sums = sums.tile([PARTS, GROUP], F32, name="column_sums")
+    column_sums = sums.tile([PARTS, width], F32, name="column_sums")
     nc.tensor.matmul(column_sums[:], ones[:], total[:], start=True, stop=True)
-    rms = work.tile([PARTS, GROUP], F32, name="rms")
+    rms = work.tile([PARTS, width], F32, name="rms")
     nc.scalar.activation(rms[:], column_sums[:], ACT.Sqrt, scale=1.0 / CHANNELS)
     nc.vector.tensor_scalar_add(rms[:], rms[:], EPS)
-    inverse = work.tile([PARTS, GROUP], F32, name="inverse")
+    inverse = work.tile([PARTS, width], F32, name="inverse")
     nc.vector.reciprocal(inverse[:], rms[:])
     normal = []
     for k in range(BLOCKS):
-        block = held.tile([PARTS, GROUP], BF16, name=f"normal_{label}_{k}")
+        block = held.tile([PARTS, width], BF16, name=f"normal_{label}_{k}")
         nc.vector.tensor_tensor(block[:], raw[k][:], inverse[:], ALU.mult)
         normal.append(block)
     return normal
 
 
-def project(nc, banks, weights, normal, m):
-    bank = banks.tile([PARTS, GROUP], F32, name="bank")
+def project(nc, banks, weights, normal, width, m):
+    bank = banks.tile([PARTS, width], F32, name="bank")
     for k in range(BLOCKS):
         nc.tensor.matmul(
             bank[:],
@@ -77,19 +81,30 @@ def tile_mtp_kernel(tc, emb, hidden, w_fut, w_hid, b, offs, out):
     nc = tc.nc
     with (
         tc.tile_pool(name="held", bufs=1) as held,
-        tc.tile_pool(name="work", bufs=3) as work,
-        tc.psum_pool(name="sums", bufs=2) as sums,
-        tc.psum_pool(name="banks", bufs=6) as banks,
+        tc.tile_pool(name="work", bufs=WORK_BUFS) as work,
+        tc.psum_pool(name="sums", bufs=SUM_BANKS) as sums,
+        tc.psum_pool(name="banks", bufs=PRODUCT_BANKS) as banks,
     ):
-        raw_hidden = load_columns(nc, held, hidden, 0, "hidden")
+        q_blocks = [held.tile([PARTS, POSITIONS], F32, name=f"q_{m}") for m in range(BLOCKS)]
+        p_blocks = [held.tile([PARTS, WORDS], F32, name=f"p_{m}") for m in range(BLOCKS)]
+
+        raw_emb0 = load_columns(nc, held, emb, 0, FIRST_THIRD, "emb0")
         offsets = held.tile([PARTS, POSITIONS // 16], U16, name="offsets")
         nc.sync.dma_start(offsets[:], offs)
         b_rows = held.tile([BLOCKS, PARTS], F32, name="b_rows")
         nc.sync.dma_start(b_rows[:], b.rearrange("(m p) o -> m (p o)", p=PARTS))
-        weights_hid = load_weights(nc, held, w_hid, "hid")
-        raw_emb = [load_columns(nc, held, emb, 0, "emb0")]
         weights_fut = load_weights(nc, held, w_fut, "fut")
-        raw_emb.append(load_columns(nc, held, emb, GROUP, "emb1"))
+        raw_hidden = load_columns(nc, held, hidden, 0, POSITIONS, "hidden")
+        weights_hid = load_weights(nc, held, w_hid, "hid")
+        raw_emb1 = load_columns(nc, held, emb, FIRST_THIRD, THIRD, "emb1")
+        raw_emb2 = load_columns(nc, held, emb, FIRST_THIRD + THIRD, THIRD, "emb2")
+
+        groups = [
+            ("emb0", raw_emb0, 0, FIRST_THIRD, weights_fut, p_blocks),
+            ("hidden", raw_hidden, 0, POSITIONS, weights_hid, q_blocks),
+            ("emb1", raw_emb1, FIRST_THIRD, THIRD, weights_fut, p_blocks),
+            ("emb2", raw_emb2, FIRST_THIRD + THIRD, THIRD, weights_fut, p_blocks),
+        ]
 
         ones = held.tile([PARTS, PARTS], F32, name="ones")
         nc.vector.memset(ones[:], 1.0)
@@ -101,26 +116,22 @@ def tile_mtp_kernel(tc, emb, hidden, w_fut, w_hid, b, offs, out):
         bias = held.tile([PARTS, BLOCKS], F32, name="bias")
         nc.vector.tensor_copy(bias[:], turned[:])
 
-        normal_hidden = normalise(nc, held, work, sums, ones, raw_hidden, "hidden")
-        normal_emb = [normalise(nc, held, work, sums, ones, raw_emb[0], "emb0")]
-
-        q_blocks = []
-        for m in range(BLOCKS):
-            bank = project(nc, banks, weights_hid, normal_hidden, m)
-            q_block = held.tile([PARTS, POSITIONS], F32, name=f"q_{m}")
-            nc.scalar.activation(q_block[:], bank[:], ACT.Identity, bias=bias[:, m : m + 1])
-            q_blocks.append(q_block)
-
-        normal_emb.append(normalise(nc, held, work, sums, ones, raw_emb[1], "emb1"))
-
-        p_blocks = [held.tile([PARTS, WORDS], F32, name=f"p_{m}") for m in range(BLOCKS)]
-        for half in range(WORDS // GROUP):
-            for m in range(BLOCKS):
-                bank = project(nc, banks, weights_fut, normal_emb[half], m)
-                nc.scalar.activation(
-                    p_blocks[m][:, half * GROUP : (half + 1) * GROUP], bank[:], ACT.Copy
+        normals = [normalise(nc, held, work, sums, ones, raw_emb0, FIRST_THIRD, "emb0")]
+        for g, (label, raw, first, width, weights, target) in enumerate(groups):
+            last_group = g == len(groups) - 1
+            if not last_group:
+                next_label, next_raw, next_first, next_width, next_weights, next_target = groups[g + 1]
+                normals.append(
+                    normalise(nc, held, work, sums, ones, next_raw, next_width, next_label)
                 )
-                if half == WORDS // GROUP - 1:
+            for m in range(BLOCKS):
+                bank = project(nc, banks, weights, normals[g], width, m)
+                columns = target[m][:, first : first + width]
+                if target is q_blocks:
+                    nc.scalar.activation(columns, bank[:], ACT.Identity, bias=bias[:, m : m + 1])
+                else:
+                    nc.scalar.activation(columns, bank[:], ACT.Copy)
+                if last_group:
                     merged = work.tile([PARTS, POSITIONS], F32, name="merged")
                     nc.vector.tensor_tensor(
                         merged[:], p_blocks[m][:].indirect(offsets[:]), q_blocks[m][:], ALU.add

@@ -16,6 +16,8 @@ EPS = 1e-8
 
 THIRD = WORDS // 3 // 16 * 16
 FIRST_THIRD = WORDS - 2 * THIRD
+LAST_POSITIONS = 128
+MOST_POSITIONS = POSITIONS - LAST_POSITIONS
 
 WORK_BUFS = 3
 SUM_BANKS = 2
@@ -94,17 +96,23 @@ def tile_mtp_kernel(tc, emb, hidden, w_fut, w_hid, b, offs, out):
         b_rows = held.tile([BLOCKS, PARTS], F32, name="b_rows")
         nc.sync.dma_start(b_rows[:], b.rearrange("(m p) o -> m (p o)", p=PARTS))
         weights_fut = load_weights(nc, held, w_fut, "fut")
-        raw_hidden = load_columns(nc, held, hidden, 0, POSITIONS, "hidden")
+        raw_hidden0 = load_columns(nc, held, hidden, 0, MOST_POSITIONS, "hidden0")
         weights_hid = load_weights(nc, held, w_hid, "hid")
         raw_emb1 = load_columns(nc, held, emb, FIRST_THIRD, THIRD, "emb1")
         raw_emb2 = load_columns(nc, held, emb, FIRST_THIRD + THIRD, THIRD, "emb2")
+        raw_hidden1 = load_columns(nc, held, hidden, MOST_POSITIONS, LAST_POSITIONS, "hidden1")
 
         groups = [
             ("emb0", raw_emb0, 0, FIRST_THIRD, weights_fut, p_blocks),
-            ("hidden", raw_hidden, 0, POSITIONS, weights_hid, q_blocks),
+            ("hidden0", raw_hidden0, 0, MOST_POSITIONS, weights_hid, q_blocks),
             ("emb1", raw_emb1, FIRST_THIRD, THIRD, weights_fut, p_blocks),
             ("emb2", raw_emb2, FIRST_THIRD + THIRD, THIRD, weights_fut, p_blocks),
+            ("hidden1", raw_hidden1, MOST_POSITIONS, LAST_POSITIONS, weights_hid, q_blocks),
         ]
+        ready_positions = {
+            "emb2": (0, MOST_POSITIONS),
+            "hidden1": (MOST_POSITIONS, LAST_POSITIONS),
+        }
 
         ones = held.tile([PARTS, PARTS], F32, name="ones")
         nc.vector.memset(ones[:], 1.0)
@@ -131,9 +139,15 @@ def tile_mtp_kernel(tc, emb, hidden, w_fut, w_hid, b, offs, out):
                     nc.scalar.activation(columns, bank[:], ACT.Identity, bias=bias[:, m : m + 1])
                 else:
                     nc.scalar.activation(columns, bank[:], ACT.Copy)
-                if last_group:
-                    merged = work.tile([PARTS, POSITIONS], F32, name="merged")
+                if label in ready_positions:
+                    position, count = ready_positions[label]
+                    merged = held.tile([PARTS, count], F32, name=f"merged_{label}_{m}")
                     nc.vector.tensor_tensor(
-                        merged[:], p_blocks[m][:].indirect(offsets[:]), q_blocks[m][:], ALU.add
+                        merged[:],
+                        p_blocks[m][:].indirect(offsets[:, position // 16 : (position + count) // 16]),
+                        q_blocks[m][:, position : position + count],
+                        ALU.add,
                     )
-                    nc.sync.dma_start(out[m * PARTS : (m + 1) * PARTS, :], merged[:])
+                    nc.sync.dma_start(
+                        out[m * PARTS : (m + 1) * PARTS, position : position + count], merged[:]
+                    )

@@ -20,6 +20,7 @@ LAST_POSITIONS = 128
 MOST_POSITIONS = POSITIONS - LAST_POSITIONS
 
 WORK_BUFS = 3
+SQUARE_BUFS = 2 * BLOCKS
 SUM_BANKS = 2
 PRODUCT_BANKS = 8 - SUM_BANKS
 
@@ -44,11 +45,11 @@ def load_weights(nc, pool, source, label):
     return weights
 
 
-def normalise(nc, held, work, sums, ones, raw, width, label):
+def normalise(nc, held, work, square_ring, sums, ones, raw, width, label):
     total = work.tile([PARTS, width], F32, name="total")
     nc.scalar.activation(total[:], raw[0][:], ACT.Square)
     for k in range(1, BLOCKS):
-        squares = work.tile([PARTS, width], F32, name="squares")
+        squares = square_ring.tile([PARTS, width], F32, name="squares")
         nc.scalar.activation(squares[:], raw[k][:], ACT.Square)
         nc.vector.tensor_tensor(total[:], total[:], squares[:], ALU.add)
     column_sums = sums.tile([PARTS, width], F32, name="column_sums")
@@ -84,6 +85,7 @@ def tile_mtp_kernel(tc, emb, hidden, w_fut, w_hid, b, offs, out):
     with (
         tc.tile_pool(name="held", bufs=1) as held,
         tc.tile_pool(name="work", bufs=WORK_BUFS) as work,
+        tc.tile_pool(name="square_ring", bufs=SQUARE_BUFS) as square_ring,
         tc.psum_pool(name="sums", bufs=SUM_BANKS) as sums,
         tc.psum_pool(name="banks", bufs=PRODUCT_BANKS) as banks,
     ):
@@ -124,13 +126,13 @@ def tile_mtp_kernel(tc, emb, hidden, w_fut, w_hid, b, offs, out):
         bias = held.tile([PARTS, BLOCKS], F32, name="bias")
         nc.vector.tensor_copy(bias[:], turned[:])
 
-        normals = [normalise(nc, held, work, sums, ones, raw_emb0, FIRST_THIRD, "emb0")]
+        normals = [normalise(nc, held, work, square_ring, sums, ones, raw_emb0, FIRST_THIRD, "emb0")]
         for g, (label, raw, first, width, weights, target) in enumerate(groups):
             last_group = g == len(groups) - 1
             if not last_group:
                 next_label, next_raw, next_first, next_width, next_weights, next_target = groups[g + 1]
                 normals.append(
-                    normalise(nc, held, work, sums, ones, next_raw, next_width, next_label)
+                    normalise(nc, held, work, square_ring, sums, ones, next_raw, next_width, next_label)
                 )
             for m in range(BLOCKS):
                 bank = project(nc, banks, weights, normals[g], width, m)

@@ -24,6 +24,9 @@ SQUARE_BUFS = 2 * BLOCKS
 SUM_BANKS = 2
 PRODUCT_BANKS = 8 - SUM_BANKS
 
+ONE_PART = (tuple(range(BLOCKS)),)
+FIRST_PARTS = ((0, 1, 2, 3), (4, 5, 6), (7,))
+
 FLOPS = 2 * CHANNELS * CHANNELS * (WORDS + POSITIONS)
 
 
@@ -45,15 +48,18 @@ def load_weights(nc, pool, source, label):
     return weights
 
 
-def normalise(nc, held, work, square_ring, sums, ones, raw, width, label):
-    total = work.tile([PARTS, width], F32, name="total")
-    nc.scalar.activation(total[:], raw[0][:], ACT.Square)
-    for k in range(1, BLOCKS):
-        squares = square_ring.tile([PARTS, width], F32, name="squares")
-        nc.scalar.activation(squares[:], raw[k][:], ACT.Square)
-        nc.vector.tensor_tensor(total[:], total[:], squares[:], ALU.add)
+def normalise(nc, held, work, square_ring, sums, ones, raw, width, label, parts):
     column_sums = sums.tile([PARTS, width], F32, name="column_sums")
-    nc.tensor.matmul(column_sums[:], ones[:], total[:], start=True, stop=True)
+    for part in parts:
+        total = work.tile([PARTS, width], F32, name="total")
+        nc.scalar.activation(total[:], raw[part[0]][:], ACT.Square)
+        for k in part[1:]:
+            squares = square_ring.tile([PARTS, width], F32, name="squares")
+            nc.scalar.activation(squares[:], raw[k][:], ACT.Square)
+            nc.vector.tensor_tensor(total[:], total[:], squares[:], ALU.add)
+        nc.tensor.matmul(
+            column_sums[:], ones[:], total[:], start=(part is parts[0]), stop=(part is parts[-1])
+        )
     rms = work.tile([PARTS, width], F32, name="rms")
     nc.scalar.activation(rms[:], column_sums[:], ACT.Sqrt, scale=1.0 / CHANNELS)
     nc.vector.tensor_scalar_add(rms[:], rms[:], EPS)
@@ -126,13 +132,13 @@ def tile_mtp_kernel(tc, emb, hidden, w_fut, w_hid, b, offs, out):
         bias = held.tile([PARTS, BLOCKS], F32, name="bias")
         nc.vector.tensor_copy(bias[:], turned[:])
 
-        normals = [normalise(nc, held, work, square_ring, sums, ones, raw_emb0, FIRST_THIRD, "emb0")]
+        normals = [normalise(nc, held, work, square_ring, sums, ones, raw_emb0, FIRST_THIRD, "emb0", FIRST_PARTS)]
         for g, (label, raw, first, width, weights, target) in enumerate(groups):
             last_group = g == len(groups) - 1
             if not last_group:
                 next_label, next_raw, next_first, next_width, next_weights, next_target = groups[g + 1]
                 normals.append(
-                    normalise(nc, held, work, square_ring, sums, ones, next_raw, next_width, next_label)
+                    normalise(nc, held, work, square_ring, sums, ones, next_raw, next_width, next_label, ONE_PART)
                 )
             for m in range(BLOCKS):
                 bank = project(nc, banks, weights, normals[g], width, m)

@@ -25,7 +25,7 @@ SUM_BANKS = 2
 PRODUCT_BANKS = 8 - SUM_BANKS
 
 ONE_PART = (tuple(range(BLOCKS)),)
-FIRST_PARTS = ((0, 1, 2, 3), (4, 5, 6), (7,))
+FIRST_PARTS = ((0, 1, 2, 3, 4), (5, 6, 7))
 
 FLOPS = 2 * CHANNELS * CHANNELS * (WORDS + POSITIONS)
 

@@ -12,12 +12,22 @@ CHANNELS = 1024
 WORDS = 1024
 POSITIONS = 512
 BLOCKS = CHANNELS // PARTS
+HALF = CHANNELS // 2
+BLOCKS_IN_LOAD = BLOCKS // 2
 EPS = 1e-8
 
-THIRD = WORDS // 3 // 16 * 16
-FIRST_THIRD = WORDS - 2 * THIRD
-LAST_POSITIONS = 128
-MOST_POSITIONS = POSITIONS - LAST_POSITIONS
+FLOOR = 1e-30
+SUM_SCALE = 2.0**-36
+MEAN_SCALE = 1.0 / (SUM_SCALE * CHANNELS)
+
+GROUPS = (
+    ("emb", 0, 128),
+    ("emb", 128, 256),
+    ("hidden", 0, 384),
+    ("emb", 384, 320),
+    ("emb", 704, 320),
+    ("hidden", 384, 128),
+)
 
 WORK_BUFS = 3
 SQUARE_BUFS = 2 * BLOCKS
@@ -32,53 +42,66 @@ FLOPS = 2 * CHANNELS * CHANNELS * (WORDS + POSITIONS)
 
 def load_columns(nc, pool, source, first, width, label):
     raw = []
-    for k in range(BLOCKS):
-        block = pool.tile([PARTS, width], F32, name=f"raw_{label}_{k}")
-        nc.sync.dma_start(block[:], source[k * PARTS : (k + 1) * PARTS, first : first + width])
-        raw.append(block)
+    for k in range(0, BLOCKS, BLOCKS_IN_LOAD):
+        blocks = pool.tile([PARTS, BLOCKS_IN_LOAD, width], F32, name=f"raw_{label}_{k}")
+        rows = source[k * PARTS : (k + BLOCKS_IN_LOAD) * PARTS, first : first + width]
+        nc.sync.dma_start(blocks[:], rows.rearrange("(k p) s -> p k s", p=PARTS))
+        raw.extend([blocks[:, i, :] for i in range(BLOCKS_IN_LOAD)])
     return raw
 
 
-def load_weights(nc, pool, source, label):
-    weights = []
-    for k in range(BLOCKS):
-        block = pool.tile([PARTS, CHANNELS], BF16, name=f"w_{label}_{k}")
-        nc.sync.dma_start(block[:], source[k * PARTS : (k + 1) * PARTS, :])
-        weights.append(block)
+def load_weights(nc, pool, source, half, label):
+    weights = pool.tile([PARTS, BLOCKS, HALF], BF16, name=f"w_{label}_{half}")
+    columns = source[:, half * HALF : (half + 1) * HALF]
+    nc.sync.dma_start(weights[:], columns.rearrange("(k p) m -> p k m", p=PARTS))
     return weights
 
 
-def normalise(nc, held, work, square_ring, sums, ones, raw, width, label, parts):
+def normalise(nc, held, work, square_ring, sums, consts, raw, width, label, parts):
     column_sums = sums.tile([PARTS, width], F32, name="column_sums")
     for part in parts:
         total = work.tile([PARTS, width], F32, name="total")
-        nc.scalar.activation(total[:], raw[part[0]][:], ACT.Square)
+        nc.scalar.activation(total[:], raw[part[0]], ACT.Square)
         for k in part[1:]:
             squares = square_ring.tile([PARTS, width], F32, name="squares")
-            nc.scalar.activation(squares[:], raw[k][:], ACT.Square)
+            nc.scalar.activation(squares[:], raw[k], ACT.Square)
             nc.vector.tensor_tensor(total[:], total[:], squares[:], ALU.add)
         nc.tensor.matmul(
-            column_sums[:], ones[:], total[:], start=(part is parts[0]), stop=(part is parts[-1])
+            column_sums[:], consts["summing"][:], total[:], start=(part is parts[0]), stop=(part is parts[-1])
         )
-    rms = work.tile([PARTS, width], F32, name="rms")
-    nc.scalar.activation(rms[:], column_sums[:], ACT.Sqrt, scale=1.0 / CHANNELS)
-    nc.vector.tensor_scalar_add(rms[:], rms[:], EPS)
+    inverse_root = work.tile([PARTS, width], F32, name="inverse_root")
+    nc.scalar.activation(
+        inverse_root[:], column_sums[:], ACT.Abs_reciprocal_sqrt, scale=MEAN_SCALE, bias=consts["floor"][:]
+    )
+    root_squared = work.tile([PARTS, width], F32, name="root_squared")
+    nc.vector.scalar_tensor_tensor(
+        root_squared[:], inverse_root[:], 1.0 / (2.0 * EPS), column_sums[:], ALU.add, ALU.mult
+    )
     inverse = work.tile([PARTS, width], F32, name="inverse")
-    nc.vector.reciprocal(inverse[:], rms[:])
+    nc.scalar.activation(
+        inverse[:],
+        root_squared[:],
+        ACT.Abs_reciprocal_sqrt,
+        scale=2.0 * EPS * MEAN_SCALE,
+        bias=consts["eps_squared"][:],
+    )
     normal = []
     for k in range(BLOCKS):
         block = held.tile([PARTS, width], BF16, name=f"normal_{label}_{k}")
-        nc.vector.tensor_tensor(block[:], raw[k][:], inverse[:], ALU.mult)
+        nc.vector.tensor_tensor(block[:], raw[k], inverse[:], ALU.mult)
         normal.append(block)
     return normal
 
 
-def project(nc, banks, weights, normal, width, m):
+def project(nc, banks, weight_halves, normal, width, m):
+    blocks_in_half = BLOCKS // 2
+    weights = weight_halves[m // blocks_in_half]
+    column = m % blocks_in_half * PARTS
     bank = banks.tile([PARTS, width], F32, name="bank")
     for k in range(BLOCKS):
         nc.tensor.matmul(
             bank[:],
-            weights[k][:, m * PARTS : (m + 1) * PARTS],
+            weights[:, k, column : column + PARTS],
             normal[k][:],
             start=(k == 0),
             stop=(k == BLOCKS - 1),
@@ -97,33 +120,37 @@ def tile_mtp_kernel(tc, emb, hidden, w_fut, w_hid, b, offs, out):
     ):
         q_blocks = [held.tile([PARTS, POSITIONS], F32, name=f"q_{m}") for m in range(BLOCKS)]
         p_blocks = [held.tile([PARTS, WORDS], F32, name=f"p_{m}") for m in range(BLOCKS)]
+        sources = {"emb": emb, "hidden": hidden}
+        targets = {"emb": p_blocks, "hidden": q_blocks}
 
-        raw_emb0 = load_columns(nc, held, emb, 0, FIRST_THIRD, "emb0")
+        raws = []
+
+        def load_group():
+            source, first, width = GROUPS[len(raws)]
+            raws.append(load_columns(nc, held, sources[source], first, width, f"group{len(raws)}"))
+
+        load_group()
         offsets = held.tile([PARTS, POSITIONS // 16], U16, name="offsets")
         nc.sync.dma_start(offsets[:], offs)
         b_rows = held.tile([BLOCKS, PARTS], F32, name="b_rows")
         nc.sync.dma_start(b_rows[:], b.rearrange("(m p) o -> m (p o)", p=PARTS))
-        weights_fut = load_weights(nc, held, w_fut, "fut")
-        raw_hidden0 = load_columns(nc, held, hidden, 0, MOST_POSITIONS, "hidden0")
-        weights_hid = load_weights(nc, held, w_hid, "hid")
-        raw_emb1 = load_columns(nc, held, emb, FIRST_THIRD, THIRD, "emb1")
-        raw_emb2 = load_columns(nc, held, emb, FIRST_THIRD + THIRD, THIRD, "emb2")
-        raw_hidden1 = load_columns(nc, held, hidden, MOST_POSITIONS, LAST_POSITIONS, "hidden1")
+        fut_first = load_weights(nc, held, w_fut, 0, "fut")
+        load_group()
+        fut_second = load_weights(nc, held, w_fut, 1, "fut")
+        load_group()
+        hid_first = load_weights(nc, held, w_hid, 0, "hid")
+        hid_second = load_weights(nc, held, w_hid, 1, "hid")
+        while len(raws) < len(GROUPS):
+            load_group()
+        weights = {"emb": (fut_first, fut_second), "hidden": (hid_first, hid_second)}
 
-        groups = [
-            ("emb0", raw_emb0, 0, FIRST_THIRD, weights_fut, p_blocks),
-            ("hidden0", raw_hidden0, 0, MOST_POSITIONS, weights_hid, q_blocks),
-            ("emb1", raw_emb1, FIRST_THIRD, THIRD, weights_fut, p_blocks),
-            ("emb2", raw_emb2, FIRST_THIRD + THIRD, THIRD, weights_fut, p_blocks),
-            ("hidden1", raw_hidden1, MOST_POSITIONS, LAST_POSITIONS, weights_hid, q_blocks),
-        ]
-        ready_positions = {
-            "emb2": (0, MOST_POSITIONS),
-            "hidden1": (MOST_POSITIONS, LAST_POSITIONS),
-        }
-
-        ones = held.tile([PARTS, PARTS], F32, name="ones")
-        nc.vector.memset(ones[:], 1.0)
+        summing = held.tile([PARTS, PARTS], F32, name="summing")
+        nc.vector.memset(summing[:], SUM_SCALE)
+        floor = held.tile([PARTS, 1], F32, name="floor")
+        nc.vector.memset(floor[:], FLOOR)
+        eps_squared = held.tile([PARTS, 1], F32, name="eps_squared")
+        nc.vector.memset(eps_squared[:], EPS * EPS)
+        consts = {"summing": summing, "floor": floor, "eps_squared": eps_squared}
 
         identity = held.tile([BLOCKS, BLOCKS], F32, name="identity")
         make_identity(nc, identity[:])
@@ -132,24 +159,32 @@ def tile_mtp_kernel(tc, emb, hidden, w_fut, w_hid, b, offs, out):
         bias = held.tile([PARTS, BLOCKS], F32, name="bias")
         nc.vector.tensor_copy(bias[:], turned[:])
 
-        normals = [normalise(nc, held, work, square_ring, sums, ones, raw_emb0, FIRST_THIRD, "emb0", FIRST_PARTS)]
-        for g, (label, raw, first, width, weights, target) in enumerate(groups):
-            last_group = g == len(groups) - 1
-            if not last_group:
-                next_label, next_raw, next_first, next_width, next_weights, next_target = groups[g + 1]
-                normals.append(
-                    normalise(nc, held, work, square_ring, sums, ones, next_raw, next_width, next_label, ONE_PART)
-                )
+        last_emb = max(g for g, group in enumerate(GROUPS) if group[0] == "emb")
+        early_positions = sum(width for source, first, width in GROUPS[:last_emb] if source == "hidden")
+
+        normals = []
+
+        def normalise_group():
+            g = len(normals)
+            parts = FIRST_PARTS if g == 0 else ONE_PART
+            normals.append(
+                normalise(nc, held, work, square_ring, sums, consts, raws[g], GROUPS[g][2], f"group{g}", parts)
+            )
+
+        normalise_group()
+        for g, (source, first, width) in enumerate(GROUPS):
+            if g + 1 < len(GROUPS):
+                normalise_group()
             for m in range(BLOCKS):
-                bank = project(nc, banks, weights, normals[g], width, m)
-                columns = target[m][:, first : first + width]
-                if target is q_blocks:
+                bank = project(nc, banks, weights[source], normals[g], width, m)
+                columns = targets[source][m][:, first : first + width]
+                if source == "hidden":
                     nc.scalar.activation(columns, bank[:], ACT.Identity, bias=bias[:, m : m + 1])
                 else:
                     nc.scalar.activation(columns, bank[:], ACT.Copy)
-                if label in ready_positions:
-                    position, count = ready_positions[label]
-                    merged = held.tile([PARTS, count], F32, name=f"merged_{label}_{m}")
+                if g >= last_emb:
+                    position, count = (0, early_positions) if g == last_emb else (first, width)
+                    merged = held.tile([PARTS, count], F32, name=f"merged_{g}_{m}")
                     nc.vector.tensor_tensor(
                         merged[:],
                         p_blocks[m][:].indirect(offsets[:, position // 16 : (position + count) // 16]),

@@ -1,5 +1,4 @@
 import concourse.mybir as mybir
-from concourse.masks import make_identity
 
 F32 = mybir.dt.float32
 BF16 = mybir.dt.bfloat16
@@ -13,7 +12,7 @@ WORDS = 1024
 POSITIONS = 512
 BLOCKS = CHANNELS // PARTS
 HALF = CHANNELS // 2
-BLOCKS_IN_LOAD = BLOCKS // 2
+LOAD_BYTES = 256 * 1024
 EPS = 1e-8
 
 FLOOR = 1e-30
@@ -23,9 +22,9 @@ MEAN_SCALE = 1.0 / (SUM_SCALE * CHANNELS)
 GROUPS = (
     ("emb", 0, 128),
     ("emb", 128, 256),
-    ("hidden", 0, 384),
     ("emb", 384, 320),
     ("emb", 704, 320),
+    ("hidden", 0, 384),
     ("hidden", 384, 128),
 )
 
@@ -35,25 +34,30 @@ SUM_BANKS = 2
 PRODUCT_BANKS = 8 - SUM_BANKS
 
 ONE_PART = (tuple(range(BLOCKS)),)
-FIRST_PARTS = ((0, 1, 2, 3, 4), (5, 6, 7))
+FIRST_PARTS = ((0, 1, 2, 3), (4, 5, 6, 7))
 
 FLOPS = 2 * CHANNELS * CHANNELS * (WORDS + POSITIONS)
 
 
 def load_columns(nc, pool, source, first, width, label):
     raw = []
-    for k in range(0, BLOCKS, BLOCKS_IN_LOAD):
-        blocks = pool.tile([PARTS, BLOCKS_IN_LOAD, width], F32, name=f"raw_{label}_{k}")
-        rows = source[k * PARTS : (k + BLOCKS_IN_LOAD) * PARTS, first : first + width]
+    count = max(2, LOAD_BYTES // (PARTS * width * 4))
+    for k in range(0, BLOCKS, count):
+        blocks = pool.tile([PARTS, count, width], F32, name=f"raw_{label}_{k}")
+        rows = source[k * PARTS : (k + count) * PARTS, first : first + width]
         nc.sync.dma_start(blocks[:], rows.rearrange("(k p) s -> p k s", p=PARTS))
-        raw.extend([blocks[:, i, :] for i in range(BLOCKS_IN_LOAD)])
+        raw.extend([blocks[:, i, :] for i in range(count)])
     return raw
 
 
 def load_weights(nc, pool, source, half, label):
-    weights = pool.tile([PARTS, BLOCKS, HALF], BF16, name=f"w_{label}_{half}")
-    columns = source[:, half * HALF : (half + 1) * HALF]
-    nc.sync.dma_start(weights[:], columns.rearrange("(k p) m -> p k m", p=PARTS))
+    weights = []
+    count = LOAD_BYTES // (PARTS * HALF * 2)
+    for k in range(0, BLOCKS, count):
+        blocks = pool.tile([PARTS, count, HALF], BF16, name=f"w_{label}_{half}_{k}")
+        rows = source[k * PARTS : (k + count) * PARTS, half * HALF : (half + 1) * HALF]
+        nc.sync.dma_start(blocks[:], rows.rearrange("(k p) m -> p k m", p=PARTS))
+        weights.extend([blocks[:, i, :] for i in range(count)])
     return weights
 
 
@@ -101,7 +105,7 @@ def project(nc, banks, weight_halves, normal, width, m):
     for k in range(BLOCKS):
         nc.tensor.matmul(
             bank[:],
-            weights[:, k, column : column + PARTS],
+            weights[k][:, column : column + PARTS],
             normal[k][:],
             start=(k == 0),
             stop=(k == BLOCKS - 1),
@@ -130,18 +134,19 @@ def tile_mtp_kernel(tc, emb, hidden, w_fut, w_hid, b, offs, out):
             raws.append(load_columns(nc, held, sources[source], first, width, f"group{len(raws)}"))
 
         load_group()
+        load_group()
+        fut_first = load_weights(nc, held, w_fut, 0, "fut")
+        fut_second = load_weights(nc, held, w_fut, 1, "fut")
+        load_group()
+        load_group()
         offsets = held.tile([PARTS, POSITIONS // 16], U16, name="offsets")
         nc.sync.dma_start(offsets[:], offs)
-        b_rows = held.tile([BLOCKS, PARTS], F32, name="b_rows")
-        nc.sync.dma_start(b_rows[:], b.rearrange("(m p) o -> m (p o)", p=PARTS))
-        fut_first = load_weights(nc, held, w_fut, 0, "fut")
-        load_group()
-        fut_second = load_weights(nc, held, w_fut, 1, "fut")
+        bias = held.tile([PARTS, BLOCKS], F32, name="bias")
+        nc.sync.dma_start(bias[:], b.rearrange("(m p) o -> p (m o)", p=PARTS))
         load_group()
         hid_first = load_weights(nc, held, w_hid, 0, "hid")
         hid_second = load_weights(nc, held, w_hid, 1, "hid")
-        while len(raws) < len(GROUPS):
-            load_group()
+        load_group()
         weights = {"emb": (fut_first, fut_second), "hidden": (hid_first, hid_second)}
 
         summing = held.tile([PARTS, PARTS], F32, name="summing")
@@ -151,16 +156,6 @@ def tile_mtp_kernel(tc, emb, hidden, w_fut, w_hid, b, offs, out):
         eps_squared = held.tile([PARTS, 1], F32, name="eps_squared")
         nc.vector.memset(eps_squared[:], EPS * EPS)
         consts = {"summing": summing, "floor": floor, "eps_squared": eps_squared}
-
-        identity = held.tile([BLOCKS, BLOCKS], F32, name="identity")
-        make_identity(nc, identity[:])
-        turned = banks.tile([PARTS, BLOCKS], F32, name="bank")
-        nc.tensor.matmul(turned[:], b_rows[:], identity[:], start=True, stop=True)
-        bias = held.tile([PARTS, BLOCKS], F32, name="bias")
-        nc.vector.tensor_copy(bias[:], turned[:])
-
-        last_emb = max(g for g, group in enumerate(GROUPS) if group[0] == "emb")
-        early_positions = sum(width for source, first, width in GROUPS[:last_emb] if source == "hidden")
 
         normals = []
 
@@ -180,17 +175,13 @@ def tile_mtp_kernel(tc, emb, hidden, w_fut, w_hid, b, offs, out):
                 columns = targets[source][m][:, first : first + width]
                 if source == "hidden":
                     nc.scalar.activation(columns, bank[:], ACT.Identity, bias=bias[:, m : m + 1])
-                else:
-                    nc.scalar.activation(columns, bank[:], ACT.Copy)
-                if g >= last_emb:
-                    position, count = (0, early_positions) if g == last_emb else (first, width)
-                    merged = held.tile([PARTS, count], F32, name=f"merged_{g}_{m}")
+                    merged = held.tile([PARTS, width], F32, name=f"merged_{g}_{m}")
                     nc.vector.tensor_tensor(
                         merged[:],
-                        p_blocks[m][:].indirect(offsets[:, position // 16 : (position + count) // 16]),
-                        q_blocks[m][:, position : position + count],
+                        p_blocks[m][:].indirect(offsets[:, first // 16 : (first + width) // 16]),
+                        columns,
                         ALU.add,
                     )
-                    nc.sync.dma_start(
-                        out[m * PARTS : (m + 1) * PARTS, position : position + count], merged[:]
-                    )
+                    nc.sync.dma_start(out[m * PARTS : (m + 1) * PARTS, first : first + width], merged[:])
+                else:
+                    nc.scalar.activation(columns, bank[:], ACT.Copy)

@@ -11,7 +11,7 @@ CHANNELS = 1024
 WORDS = 1024
 POSITIONS = 512
 BLOCKS = CHANNELS // PARTS
-HALF = CHANNELS // 2
+QUARTER = CHANNELS // 4
 LOAD_BYTES = 256 * 1024
 EPS = 1e-8
 
@@ -50,15 +50,15 @@ def load_columns(nc, pool, source, first, width, label):
     return raw
 
 
-def load_weights(nc, pool, source, half, label):
-    weights = []
-    count = LOAD_BYTES // (PARTS * HALF * 2)
+def load_weights(nc, pool, source, first, width, label):
+    blocks_in = []
+    count = LOAD_BYTES // (PARTS * width * 2)
     for k in range(0, BLOCKS, count):
-        blocks = pool.tile([PARTS, count, HALF], BF16, name=f"w_{label}_{half}_{k}")
-        rows = source[k * PARTS : (k + count) * PARTS, half * HALF : (half + 1) * HALF]
+        blocks = pool.tile([PARTS, count, width], BF16, name=f"w_{label}_{first}_{k}")
+        rows = source[k * PARTS : (k + count) * PARTS, first : first + width]
         nc.sync.dma_start(blocks[:], rows.rearrange("(k p) m -> p k m", p=PARTS))
-        weights.extend([blocks[:, i, :] for i in range(count)])
-    return weights
+        blocks_in.extend([blocks[:, i, :] for i in range(count)])
+    return [[block[:, m : m + PARTS] for block in blocks_in] for m in range(0, width, PARTS)]
 
 
 def normalise(nc, held, work, square_ring, sums, consts, raw, width, label, parts):
@@ -97,15 +97,12 @@ def normalise(nc, held, work, square_ring, sums, consts, raw, width, label, part
     return normal
 
 
-def project(nc, banks, weight_halves, normal, width, m):
-    blocks_in_half = BLOCKS // 2
-    weights = weight_halves[m // blocks_in_half]
-    column = m % blocks_in_half * PARTS
+def project(nc, banks, weights, normal, width):
     bank = banks.tile([PARTS, width], F32, name="bank")
     for k in range(BLOCKS):
         nc.tensor.matmul(
             bank[:],
-            weights[k][:, column : column + PARTS],
+            weights[k],
             normal[k][:],
             start=(k == 0),
             stop=(k == BLOCKS - 1),
@@ -135,8 +132,9 @@ def tile_mtp_kernel(tc, emb, hidden, w_fut, w_hid, b, offs, out):
 
         load_group()
         load_group()
-        fut_first = load_weights(nc, held, w_fut, 0, "fut")
-        fut_second = load_weights(nc, held, w_fut, 1, "fut")
+        weights_fut = []
+        for first in range(0, CHANNELS, QUARTER):
+            weights_fut.extend(load_weights(nc, held, w_fut, first, QUARTER, "fut"))
         load_group()
         load_group()
         offsets = held.tile([PARTS, POSITIONS // 16], U16, name="offsets")
@@ -144,10 +142,9 @@ def tile_mtp_kernel(tc, emb, hidden, w_fut, w_hid, b, offs, out):
         bias = held.tile([PARTS, BLOCKS], F32, name="bias")
         nc.sync.dma_start(bias[:], b.rearrange("(m p) o -> p (m o)", p=PARTS))
         load_group()
-        hid_first = load_weights(nc, held, w_hid, 0, "hid")
-        hid_second = load_weights(nc, held, w_hid, 1, "hid")
+        weights_hid = load_weights(nc, held, w_hid, 0, CHANNELS, "hid")
         load_group()
-        weights = {"emb": (fut_first, fut_second), "hidden": (hid_first, hid_second)}
+        weights = {"emb": weights_fut, "hidden": weights_hid}
 
         summing = held.tile([PARTS, PARTS], F32, name="summing")
         nc.vector.memset(summing[:], SUM_SCALE)
@@ -171,7 +168,7 @@ def tile_mtp_kernel(tc, emb, hidden, w_fut, w_hid, b, offs, out):
             if g + 1 < len(GROUPS):
                 normalise_group()
             for m in range(BLOCKS):
-                bank = project(nc, banks, weights[source], normals[g], width, m)
+                bank = project(nc, banks, weights[source][m], normals[g], width)
                 columns = targets[source][m][:, first : first + width]
                 if source == "hidden":
                     nc.scalar.activation(columns, bank[:], ACT.Identity, bias=bias[:, m : m + 1])

@@ -36,6 +36,8 @@ PRODUCT_BANKS = 8 - SUM_BANKS
 ONE_PART = (tuple(range(BLOCKS)),)
 FIRST_PARTS = ((0, 1, 2, 3), (4, 5, 6, 7))
 
+TOGETHER = 2
+
 FLOPS = 2 * CHANNELS * CHANNELS * (WORDS + POSITIONS)
 
 
@@ -98,16 +100,17 @@ def normalise(nc, held, work, square_ring, sums, consts, raw, width, label, part
 
 
 def project(nc, banks, weights, normal, width):
-    bank = banks.tile([PARTS, width], F32, name="bank")
+    products = [banks.tile([PARTS, width], F32, name="bank") for block in weights]
     for k in range(BLOCKS):
-        nc.tensor.matmul(
-            bank[:],
-            weights[k],
-            normal[k][:],
-            start=(k == 0),
-            stop=(k == BLOCKS - 1),
-        )
-    return bank
+        for bank, block in zip(products, weights):
+            nc.tensor.matmul(
+                bank[:],
+                block[k],
+                normal[k][:],
+                start=(k == 0),
+                stop=(k == BLOCKS - 1),
+            )
+    return products
 
 
 def tile_mtp_kernel(tc, emb, hidden, w_fut, w_hid, b, offs, out):
@@ -142,8 +145,8 @@ def tile_mtp_kernel(tc, emb, hidden, w_fut, w_hid, b, offs, out):
         bias = held.tile([PARTS, BLOCKS], F32, name="bias")
         nc.sync.dma_start(bias[:], b.rearrange("(m p) o -> p (m o)", p=PARTS))
         load_group()
-        weights_hid = load_weights(nc, held, w_hid, 0, CHANNELS, "hid")
         load_group()
+        weights_hid = load_weights(nc, held, w_hid, 0, CHANNELS, "hid")
         weights = {"emb": weights_fut, "hidden": weights_hid}
 
         summing = held.tile([PARTS, PARTS], F32, name="summing")
@@ -167,8 +170,11 @@ def tile_mtp_kernel(tc, emb, hidden, w_fut, w_hid, b, offs, out):
         for g, (source, first, width) in enumerate(GROUPS):
             if g + 1 < len(GROUPS):
                 normalise_group()
+            together = 1 if g + 1 == len(GROUPS) else TOGETHER
             for m in range(BLOCKS):
-                bank = project(nc, banks, weights[source][m], normals[g], width)
+                if m % together == 0:
+                    products = project(nc, banks, weights[source][m : m + together], normals[g], width)
+                bank = products[m % together]
                 columns = targets[source][m][:, first : first + width]
                 if source == "hidden":
                     nc.scalar.activation(columns, bank[:], ACT.Identity, bias=bias[:, m : m + 1])

@@ -13,6 +13,7 @@ POSITIONS = 512
 BLOCKS = CHANNELS // PARTS
 QUARTER = CHANNELS // 4
 LOAD_BYTES = 256 * 1024
+WEIGHT_LOAD_BYTES = 512 * 1024
 EPS = 1e-8
 
 FLOOR = 1e-30
@@ -20,10 +21,9 @@ SUM_SCALE = 2.0**-36
 MEAN_SCALE = 1.0 / (SUM_SCALE * CHANNELS)
 
 GROUPS = (
-    ("emb", 0, 128),
-    ("emb", 128, 256),
-    ("emb", 384, 320),
-    ("emb", 704, 320),
+    ("emb", 0, 192),
+    ("emb", 192, 352),
+    ("emb", 544, 480),
     ("hidden", 0, 384),
     ("hidden", 384, 128),
 )
@@ -34,9 +34,7 @@ SUM_BANKS = 2
 PRODUCT_BANKS = 8 - SUM_BANKS
 
 ONE_PART = (tuple(range(BLOCKS)),)
-FIRST_PARTS = ((0, 1, 2, 3), (4, 5, 6, 7))
-
-TOGETHER = 2
+FIRST_PARTS = ((0, 1), (2, 3), (4, 5), (6, 7))
 
 FLOPS = 2 * CHANNELS * CHANNELS * (WORDS + POSITIONS)
 
@@ -54,7 +52,7 @@ def load_columns(nc, pool, source, first, width, label):
 
 def load_weights(nc, pool, source, first, width, label):
     blocks_in = []
-    count = LOAD_BYTES // (PARTS * width * 2)
+    count = WEIGHT_LOAD_BYTES // (PARTS * width * 2)
     for k in range(0, BLOCKS, count):
         blocks = pool.tile([PARTS, count, width], BF16, name=f"w_{label}_{first}_{k}")
         rows = source[k * PARTS : (k + count) * PARTS, first : first + width]
@@ -66,14 +64,21 @@ def load_weights(nc, pool, source, first, width, label):
 def normalise(nc, held, work, square_ring, sums, consts, raw, width, label, parts):
     column_sums = sums.tile([PARTS, width], F32, name="column_sums")
     for part in parts:
-        total = work.tile([PARTS, width], F32, name="total")
-        nc.scalar.activation(total[:], raw[part[0]], ACT.Square)
-        for k in part[1:]:
+        partial_sums = []
+        for k in part:
             squares = square_ring.tile([PARTS, width], F32, name="squares")
             nc.scalar.activation(squares[:], raw[k], ACT.Square)
-            nc.vector.tensor_tensor(total[:], total[:], squares[:], ALU.add)
+            partial_sums.append(squares)
+        while len(partial_sums) > 1:
+            for left, right in zip(partial_sums[0::2], partial_sums[1::2]):
+                nc.vector.tensor_tensor(left[:], left[:], right[:], ALU.add)
+            partial_sums = partial_sums[0::2]
         nc.tensor.matmul(
-            column_sums[:], consts["summing"][:], total[:], start=(part is parts[0]), stop=(part is parts[-1])
+            column_sums[:],
+            consts["summing"][:],
+            partial_sums[0][:],
+            start=(part is parts[0]),
+            stop=(part is parts[-1]),
         )
     inverse_root = work.tile([PARTS, width], F32, name="inverse_root")
     nc.scalar.activation(
@@ -100,17 +105,16 @@ def normalise(nc, held, work, square_ring, sums, consts, raw, width, label, part
 
 
 def project(nc, banks, weights, normal, width):
-    products = [banks.tile([PARTS, width], F32, name="bank") for block in weights]
+    bank = banks.tile([PARTS, width], F32, name="bank")
     for k in range(BLOCKS):
-        for bank, block in zip(products, weights):
-            nc.tensor.matmul(
-                bank[:],
-                block[k],
-                normal[k][:],
-                start=(k == 0),
-                stop=(k == BLOCKS - 1),
-            )
-    return products
+        nc.tensor.matmul(
+            bank[:],
+            weights[k],
+            normal[k][:],
+            start=(k == 0),
+            stop=(k == BLOCKS - 1),
+        )
+    return bank
 
 
 def tile_mtp_kernel(tc, emb, hidden, w_fut, w_hid, b, offs, out):
@@ -134,19 +138,20 @@ def tile_mtp_kernel(tc, emb, hidden, w_fut, w_hid, b, offs, out):
             raws.append(load_columns(nc, held, sources[source], first, width, f"group{len(raws)}"))
 
         load_group()
-        load_group()
         weights_fut = []
-        for first in range(0, CHANNELS, QUARTER):
+        for first in (0, QUARTER):
             weights_fut.extend(load_weights(nc, held, w_fut, first, QUARTER, "fut"))
         load_group()
+        for first in (2 * QUARTER, 3 * QUARTER):
+            weights_fut.extend(load_weights(nc, held, w_fut, first, QUARTER, "fut"))
         load_group()
         offsets = held.tile([PARTS, POSITIONS // 16], U16, name="offsets")
         nc.sync.dma_start(offsets[:], offs)
         bias = held.tile([PARTS, BLOCKS], F32, name="bias")
         nc.sync.dma_start(bias[:], b.rearrange("(m p) o -> p (m o)", p=PARTS))
         load_group()
-        load_group()
         weights_hid = load_weights(nc, held, w_hid, 0, CHANNELS, "hid")
+        load_group()
         weights = {"emb": weights_fut, "hidden": weights_hid}
 
         summing = held.tile([PARTS, PARTS], F32, name="summing")
@@ -170,11 +175,8 @@ def tile_mtp_kernel(tc, emb, hidden, w_fut, w_hid, b, offs, out):
         for g, (source, first, width) in enumerate(GROUPS):
             if g + 1 < len(GROUPS):
                 normalise_group()
-            together = 1 if g + 1 == len(GROUPS) else TOGETHER
             for m in range(BLOCKS):
-                if m % together == 0:
-                    products = project(nc, banks, weights[source][m : m + together], normals[g], width)
-                bank = products[m % together]
+                bank = project(nc, banks, weights[source][m], normals[g], width)
                 columns = targets[source][m][:, first : first + width]
                 if source == "hidden":
                     nc.scalar.activation(columns, bank[:], ACT.Identity, bias=bias[:, m : m + 1])

import concourse.mybir as mybir

F32 = mybir.dt.float32
BF16 = mybir.dt.bfloat16
U16 = mybir.dt.uint16
ACT = mybir.ActivationFunctionType
ALU = mybir.AluOpType

PARTS = 128
CHANNELS = 1024
WORDS = 1024
POSITIONS = 512
BLOCKS = CHANNELS // PARTS
QUARTER = CHANNELS // 4
LOAD_BYTES = 256 * 1024
WEIGHT_LOAD_BYTES = 512 * 1024
EPS = 1e-8

FLOOR = 1e-30
SUM_SCALE = 2.0**-36
MEAN_SCALE = 1.0 / (SUM_SCALE * CHANNELS)

GROUPS = (
    ("emb", 0, 192),
    ("emb", 192, 352),
    ("emb", 544, 480),
    ("hidden", 0, 384),
    ("hidden", 384, 128),
)

WORK_BUFS = 3
SQUARE_BUFS = 2 * BLOCKS
SUM_BANKS = 2
PRODUCT_BANKS = 8 - SUM_BANKS

ONE_PART = (tuple(range(BLOCKS)),)
FIRST_PARTS = ((0, 1), (2, 3), (4, 5), (6, 7))

FLOPS = 2 * CHANNELS * CHANNELS * (WORDS + POSITIONS)


def load_columns(nc, pool, source, first, width, label):
    raw = []
    count = max(2, LOAD_BYTES // (PARTS * width * 4))
    for k in range(0, BLOCKS, count):
        blocks = pool.tile([PARTS, count, width], F32, name=f"raw_{label}_{k}")
        rows = source[k * PARTS : (k + count) * PARTS, first : first + width]
        nc.sync.dma_start(blocks[:], rows.rearrange("(k p) s -> p k s", p=PARTS))
        raw.extend([blocks[:, i, :] for i in range(count)])
    return raw


def load_weights(nc, pool, source, first, width, label):
    blocks_in = []
    count = WEIGHT_LOAD_BYTES // (PARTS * width * 2)
    for k in range(0, BLOCKS, count):
        blocks = pool.tile([PARTS, count, width], BF16, name=f"w_{label}_{first}_{k}")
        rows = source[k * PARTS : (k + count) * PARTS, first : first + width]
        nc.sync.dma_start(blocks[:], rows.rearrange("(k p) m -> p k m", p=PARTS))
        blocks_in.extend([blocks[:, i, :] for i in range(count)])
    return [[block[:, m : m + PARTS] for block in blocks_in] for m in range(0, width, PARTS)]


def normalise(nc, held, work, square_ring, sums, consts, raw, width, label, parts):
    column_sums = sums.tile([PARTS, width], F32, name="column_sums")
    for part in parts:
        partial_sums = []
        for k in part:
            squares = square_ring.tile([PARTS, width], F32, name="squares")
            nc.scalar.activation(squares[:], raw[k], ACT.Square)
            partial_sums.append(squares)
        while len(partial_sums) > 1:
            for left, right in zip(partial_sums[0::2], partial_sums[1::2]):
                nc.vector.tensor_tensor(left[:], left[:], right[:], ALU.add)
            partial_sums = partial_sums[0::2]
        nc.tensor.matmul(
            column_sums[:],
            consts["summing"][:],
            partial_sums[0][:],
            start=(part is parts[0]),
            stop=(part is parts[-1]),
        )
    inverse_root = work.tile([PARTS, width], F32, name="inverse_root")
    nc.scalar.activation(
        inverse_root[:], column_sums[:], ACT.Abs_reciprocal_sqrt, scale=MEAN_SCALE, bias=consts["floor"][:]
    )
    root_squared = work.tile([PARTS, width], F32, name="root_squared")
    nc.vector.scalar_tensor_tensor(
        root_squared[:], inverse_root[:], 1.0 / (2.0 * EPS), column_sums[:], ALU.add, ALU.mult
    )
    inverse = work.tile([PARTS, width], F32, name="inverse")
    nc.scalar.activation(
        inverse[:],
        root_squared[:],
        ACT.Abs_reciprocal_sqrt,
        scale=2.0 * EPS * MEAN_SCALE,
        bias=consts["eps_squared"][:],
    )
    normal = []
    for k in range(BLOCKS):
        block = held.tile([PARTS, width], BF16, name=f"normal_{label}_{k}")
        nc.vector.tensor_tensor(block[:], raw[k], inverse[:], ALU.mult)
        normal.append(block)
    return normal


def project(nc, banks, weights, normal, width):
    bank = banks.tile([PARTS, width], F32, name="bank")
    for k in range(BLOCKS):
        nc.tensor.matmul(
            bank[:],
            weights[k],
            normal[k][:],
            start=(k == 0),
            stop=(k == BLOCKS - 1),
        )
    return bank


def tile_mtp_kernel(tc, emb, hidden, w_fut, w_hid, b, offs, out):
    nc = tc.nc
    with (
        tc.tile_pool(name="held", bufs=1) as held,
        tc.tile_pool(name="work", bufs=WORK_BUFS) as work,
        tc.tile_pool(name="square_ring", bufs=SQUARE_BUFS) as square_ring,
        tc.psum_pool(name="sums", bufs=SUM_BANKS) as sums,
        tc.psum_pool(name="banks", bufs=PRODUCT_BANKS) as banks,
    ):
        q_blocks = [held.tile([PARTS, POSITIONS], F32, name=f"q_{m}") for m in range(BLOCKS)]
        p_blocks = [held.tile([PARTS, WORDS], F32, name=f"p_{m}") for m in range(BLOCKS)]
        sources = {"emb": emb, "hidden": hidden}
        targets = {"emb": p_blocks, "hidden": q_blocks}

        raws = []

        def load_group():
            source, first, width = GROUPS[len(raws)]
            raws.append(load_columns(nc, held, sources[source], first, width, f"group{len(raws)}"))

        load_group()
        weights_fut = []
        for first in (0, QUARTER):
            weights_fut.extend(load_weights(nc, held, w_fut, first, QUARTER, "fut"))
        load_group()
        for first in (2 * QUARTER, 3 * QUARTER):
            weights_fut.extend(load_weights(nc, held, w_fut, first, QUARTER, "fut"))
        load_group()
        offsets = held.tile([PARTS, POSITIONS // 16], U16, name="offsets")
        nc.sync.dma_start(offsets[:], offs)
        bias = held.tile([PARTS, BLOCKS], F32, name="bias")
        nc.sync.dma_start(bias[:], b.rearrange("(m p) o -> p (m o)", p=PARTS))
        load_group()
        weights_hid = load_weights(nc, held, w_hid, 0, CHANNELS, "hid")
        load_group()
        weights = {"emb": weights_fut, "hidden": weights_hid}

        summing = held.tile([PARTS, PARTS], F32, name="summing")
        nc.vector.memset(summing[:], SUM_SCALE)
        floor = held.tile([PARTS, 1], F32, name="floor")
        nc.vector.memset(floor[:], FLOOR)
        eps_squared = held.tile([PARTS, 1], F32, name="eps_squared")
        nc.vector.memset(eps_squared[:], EPS * EPS)
        consts = {"summing": summing, "floor": floor, "eps_squared": eps_squared}

        normals = []

        def normalise_group():
            g = len(normals)
            parts = FIRST_PARTS if g == 0 else ONE_PART
            normals.append(
                normalise(nc, held, work, square_ring, sums, consts, raws[g], GROUPS[g][2], f"group{g}", parts)
            )

        normalise_group()
        for g, (source, first, width) in enumerate(GROUPS):
            if g + 1 < len(GROUPS):
                normalise_group()
            for m in range(BLOCKS):
                bank = project(nc, banks, weights[source][m], normals[g], width)
                columns = targets[source][m][:, first : first + width]
                if source == "hidden":
                    nc.scalar.activation(columns, bank[:], ACT.Identity, bias=bias[:, m : m + 1])
                    merged = held.tile([PARTS, width], F32, name=f"merged_{g}_{m}")
                    nc.vector.tensor_tensor(
                        merged[:],
                        p_blocks[m][:].indirect(offsets[:, first // 16 : (first + width) // 16]),
                        columns,
                        ALU.add,
                    )
                    nc.sync.dma_start(out[m * PARTS : (m + 1) * PARTS, first : first + width], merged[:])
                else:
                    nc.scalar.activation(columns, bank[:], ACT.Copy)
